import numpy as np
import ml_dtypes


def mxq(x, axis, fmt="e4m3"):
    dtype, down = {"e4m3": (ml_dtypes.float8_e4m3fn, 7), "e5m2": (ml_dtypes.float8_e5m2, 14)}[fmt]
    v = np.moveaxis(np.asarray(x, np.float32).astype(ml_dtypes.bfloat16).astype(np.float64), axis, -1)
    blocks = v.reshape(v.shape[:-1] + (-1, 32))
    amax = np.abs(blocks).max(-1, keepdims=True)
    byte = np.maximum(np.where(amax > 0, np.frexp(amax)[1] - 1 + 127, 0) - down, 1)
    scale = np.exp2(byte - 127.0)
    codes = (blocks / scale).astype(np.float32).astype(dtype).astype(np.float64)
    return np.moveaxis((codes * scale).reshape(v.shape), -1, axis)


WIDE = False


def mx_kscale(k):
    if not WIDE:
        return np.ones(k)
    levels = np.array([10, -10, 5, -5, 0])
    a = np.random.permutation(np.resize(levels, k // 512 * 4)).reshape(k // 512, 4)
    idx = np.arange(k)
    return np.exp2(a[idx // 512, idx % 128 // 32])


BF16 = ml_dtypes.bfloat16


def bf(x):
    return np.asarray(x, np.float32).astype(BF16)


def f64(x):
    return np.asarray(x).astype(np.float64)


B, HI, WI, F, D, NH, C = 1, 32, 32, 1024, 256, 3, 16
N = HI * WI
EPS = 1e-12


def l2norm_rows(a):
    n = np.sqrt(np.sum(a * a, axis=1, keepdims=True))
    return a / np.maximum(n, EPS)


def setup_inputs():
    s = mx_kscale(F)

    def w():
        return bf(np.random.standard_normal((D, F)) / np.sqrt(F) / s[None, :])

    def b():
        return bf(np.random.standard_normal(D) * 0.2)

    return {"x": bf(np.random.standard_normal((B, F, HI, WI)) * s[None, :, None, None]),
            "W1": w(), "b1": b(), "W2": w(), "b2": b(), "W3": w(), "b3": b()}


def reference(x, W1, b1, W2, b2, W3, b3):
    xq = mxq(f64(x).reshape(F, N).T, 1, "e4m3")
    heads = [l2norm_rows((xq @ mxq(f64(W), 1, "e4m3").T) + f64(b)) for W, b in ((W1, b1), (W2, b2), (W3, b3))]
    return np.stack(heads)

@@ -1,0 +1,237 @@
+import concourse.mybir as mybir
+from concourse.masks import make_identity
+
+F32 = mybir.dt.float32
+BF16 = mybir.dt.bfloat16
+U32 = mybir.dt.uint32
+U8 = mybir.dt.uint8
+FP8X4 = mybir.dt.float8_e4m3fn_x4
+ALU = mybir.AluOpType
+ACT = mybir.ActivationFunctionType
+
+P = 128
+PACK = 4
+K_PASS = P * PACK
+FEATURES = 1024
+NODES = 1024
+DIM = 256
+HEADS = 3
+PASSES = FEATURES // K_PASS
+EPS = 1e-12
+FLOPS = 2 * NODES * FEATURES * HEADS * DIM
+
+X_CHUNK = 512
+X_CHUNKS = NODES // X_CHUNK
+X_VECTOR_NODES = 320
+PAIR = 2
+PAIRS_PER_HEAD = NODES // (PAIR * P)
+N_PAIRS = HEADS * PAIRS_PER_HEAD
+
+
+def tile_gat_pa_kernel(tc, x, W1, b1, W2, b2, W3, b3, out):
+    nc = tc.nc
+    weights = (W1, W2, W3)
+    biases = (b1, b2, b3)
+    x_rows = x.rearrange("b f i j -> (b f) (i j)")
+
+    with tc.tile_pool(name="keep", bufs=1) as keep, tc.tile_pool(
+        name="hidden_pool", bufs=6
+    ) as hidden_pool, tc.tile_pool(name="result_pool", bufs=8) as result_pool, tc.tile_pool(
+        name="stats", bufs=6
+    ) as stats, tc.psum_pool(name="wt_psum", bufs=2) as wt_psum, tc.psum_pool(
+        name="acc_psum", bufs=4
+    ) as acc_psum, tc.manual_schedule():
+        bias_rows = keep.tile([P, HEADS, DIM], BF16, name="bias_rows")
+        nc.vector.memset(bias_rows[:], 0.0)
+
+        x_raw = {}
+        w_raw = {}
+
+        def load_x(c):
+            for g in range(PASSES):
+                x_raw[g, c] = keep.tile([P, PACK, X_CHUNK], BF16, name="x_raw%d_%d" % (g, c))
+                nc.sync.dma_start(
+                    out=x_raw[g, c][:],
+                    in_=x_rows[
+                        g * K_PASS : (g + 1) * K_PASS, c * X_CHUNK : (c + 1) * X_CHUNK
+                    ].rearrange("(p t) n -> p t n", t=PACK),
+                )
+
+        def load_w(h):
+            w_raw[h] = keep.tile([P, 2 * FEATURES], BF16, name="w_raw%d" % h)
+            nc.sync.dma_start(
+                out=w_raw[h][:], in_=weights[h].rearrange("(m r) k -> m (r k)", r=2)
+            )
+
+        load_x(0)
+        for h in range(HEADS):
+            nc.sync.dma_start(
+                out=bias_rows[0:1, h, :], in_=biases[h].rearrange("(o d) -> o d", o=1)
+            )
+        load_w(0)
+        load_x(1)
+        load_w(1)
+        load_w(2)
+
+        ident = keep.tile([P, P], F32, name="ident")
+        make_identity(nc, ident[:])
+        ones = keep.tile([P, P], BF16, name="ones")
+        nc.vector.memset(ones[:], 1.0)
+        warm = keep.tile([P, 1], F32, name="warm")
+        nc.vector.memset(warm[:], 1.0)
+        nc.scalar.activation(out=warm[:], in_=warm[:], func=ACT.Sqrt)
+
+        bias_all = keep.tile([P, HEADS, DIM], F32, name="bias_all")
+        for h in range(HEADS):
+            bias_ps = acc_psum.tile([P, DIM], F32, tag="acc")
+            nc.tensor.matmul(
+                out=bias_ps[:], lhsT=ones[:], rhs=bias_rows[:, h, :], start=True, stop=True
+            )
+            nc.scalar.copy(out=bias_all[:, h, :], in_=bias_ps[:])
+
+        x_codes = keep.tile([P, PASSES, NODES], U32, name="x_codes", align_bytes=64)
+        x_scales = keep.tile([P, PASSES, NODES], U8, name="x_scales", align_bytes=64)
+        x_grouped = {}
+
+        def regroup_x(c):
+            for g in range(PASSES):
+                x_grouped[g, c] = keep.tile(
+                    [P, X_CHUNK, PACK], BF16, name="x_grouped%d_%d" % (g, c), align_bytes=64
+                )
+                dst = x_grouped[g, c][:].rearrange("p (c i) t -> p c t i", i=4)
+                src = x_raw[g, c][:].rearrange("p t (c i) -> p c t i", i=4)
+                cut = X_VECTOR_NODES // 4
+                nc.vector.tensor_copy(out=dst[:, :cut], in_=src[:, :cut])
+                nc.scalar.copy(out=dst[:, cut:], in_=src[:, cut:])
+
+        def quantise_x(c):
+            nodes = slice(c * X_CHUNK, (c + 1) * X_CHUNK)
+            for g in range(PASSES):
+                nc.vector.quantize_mx(
+                    out=x_codes[:, g, nodes].bitcast(FP8X4),
+                    scales=x_scales[:, g, nodes],
+                    in_=x_grouped[g, c][:].rearrange("p n t -> p (n t)"),
+                )
+
+        w_codes = keep.tile([P, HEADS, PASSES, DIM], U32, name="w_codes", align_bytes=64)
+        w_scales = keep.tile([P, HEADS, PASSES, DIM], U8, name="w_scales", align_bytes=64)
+        w_grouped = {}
+
+        def transpose_w(h):
+            words = w_raw[h][:].bitcast(F32).rearrange("m (r w) -> m r w", r=2)
+            w_grouped[h] = keep.tile(
+                [P, PASSES * DIM * PACK], BF16, name="w_grouped%d" % h, align_bytes=64
+            )
+            grouped_words = w_grouped[h][:].bitcast(F32).rearrange(
+                "p (g m r u) -> p g m r u", g=PASSES, r=2, u=2
+            )
+            for g in range(PASSES):
+                wt = wt_psum.tile([P, 2, 2, P], F32, tag="wt")
+                for r in range(2):
+                    for u in range(2):
+                        nc.tensor.transpose(
+                            wt[:, r, u, :],
+                            words[:, r, 256 * g + u : 256 * (g + 1) : 2],
+                            ident[:],
+                        )
+                nc.scalar.copy(
+                    out=grouped_words[:, g], in_=wt[:].rearrange("p r u m -> p m r u")
+                )
+
+        def quantise_w(h):
+            for g in range(PASSES):
+                nc.vector.quantize_mx(
+                    out=w_codes[:, h, g, :].bitcast(FP8X4),
+                    scales=w_scales[:, h, g, :],
+                    in_=w_grouped[h][:, g * DIM * PACK : (g + 1) * DIM * PACK],
+                )
+
+        hidden = {}
+        result = {}
+        sumsq = {}
+        inv_norm = {}
+
+        def project(j):
+            h, q = divmod(j, PAIRS_PER_HEAD)
+            acc = acc_psum.tile([P, PAIR, DIM], F32, tag="acc")
+            for m in range(PAIR):
+                nodes = slice((q * PAIR + m) * P, (q * PAIR + m + 1) * P)
+                for g in range(PASSES):
+                    nc.tensor.matmul_mx(
+                        out=acc[:, m, :],
+                        lhsT=x_codes[:, g, nodes].bitcast(FP8X4),
+                        lhsT_scale=x_scales[:, g, nodes],
+                        rhs=w_codes[:, h, g, :].bitcast(FP8X4),
+                        rhs_scale=w_scales[:, h, g, :],
+                        start=(g == 0),
+                        stop=(g == PASSES - 1),
+                    )
+            hidden[j] = hidden_pool.tile([P, PAIR, DIM], F32, name="hidden", tag="hidden")
+            nc.vector.tensor_tensor(
+                out=hidden[j][:],
+                in0=acc[:],
+                in1=bias_all[:, h : h + 1, :].to_broadcast([P, PAIR, DIM]),
+                op=ALU.add,
+            )
+            result[j] = result_pool.tile([P, PAIR, DIM], F32, name="result", tag="result")
+            sumsq[j] = stats.tile([P, PAIR], F32, name="sumsq", tag="sumsq")
+            for m in range(PAIR):
+                nc.scalar.activation(
+                    out=result[j][:, m, :],
+                    in_=hidden[j][:, m, :],
+                    func=ACT.Square,
+                    accum_out=sumsq[j][:, m : m + 1],
+                )
+
+        def invert_norms(j):
+            inv_sq = stats.tile([P, PAIR], F32, tag="inv_sq")
+            nc.vector.tensor_scalar(
+                out=inv_sq[:], in0=sumsq[j][:], scalar1=EPS * EPS, scalar2=None, op0=ALU.max
+            )
+            nc.vector.reciprocal(out=inv_sq[:], in_=inv_sq[:])
+            inv_norm[j] = stats.tile([P, PAIR], F32, name="inv_norm", tag="inv_norm")
+            nc.scalar.activation(out=inv_norm[j][:], in_=inv_sq[:], func=ACT.Sqrt)
+
+        def scale_and_store(j):
+            h, q = divmod(j, PAIRS_PER_HEAD)
+            nc.gpsimd.tensor_scalar(
+                out=result[j][:, 0, :],
+                in0=hidden[j][:, 0, :],
+                scalar1=inv_norm[j][:, 0:1],
+                scalar2=0.0,
+                op0=ALU.mult,
+                op1=ALU.add,
+            )
+            nc.vector.tensor_scalar(
+                out=result[j][:, 1, :],
+                in0=hidden[j][:, 1, :],
+                scalar1=inv_norm[j][:, 1:2],
+                scalar2=None,
+                op0=ALU.mult,
+            )
+            nc.sync.dma_start(
+                out=out[h, q * PAIR * P : (q + 1) * PAIR * P, :].rearrange(
+                    "(m p) d -> p m d", p=P
+                ),
+                in_=result[j][:],
+            )
+
+        regroup_x(0)
+        quantise_x(0)
+        transpose_w(0)
+        regroup_x(1)
+        quantise_w(0)
+        for step in range(N_PAIRS + 3):
+            if step < N_PAIRS:
+                project(step)
+            if 1 <= step <= N_PAIRS:
+                invert_norms(step - 1)
+            if step >= 3:
+                scale_and_store(step - 3)
+            if step == 0:
+                quantise_x(1)
+            h, q = divmod(step, PAIRS_PER_HEAD)
+            if h + 1 < HEADS and q == 1:
+                transpose_w(h + 1)
+            if h + 1 < HEADS and q == 2:
+                quantise_w(h + 1)

@@ -47,15 +47,14 @@ def tile_gat_pa_kernel(tc, x, W1, b1, W2, b2, W3, b3, out):
         x_raw = {}
         w_raw = {}
 
-        def load_x(c):
-            for g in range(PASSES):
-                x_raw[g, c] = keep.tile([P, PACK, X_CHUNK], BF16, name="x_raw%d_%d" % (g, c))
-                nc.sync.dma_start(
-                    out=x_raw[g, c][:],
-                    in_=x_rows[
-                        g * K_PASS : (g + 1) * K_PASS, c * X_CHUNK : (c + 1) * X_CHUNK
-                    ].rearrange("(p t) n -> p t n", t=PACK),
-                )
+        def load_x(g, c):
+            x_raw[g, c] = keep.tile([P, PACK, X_CHUNK], BF16, name="x_raw%d_%d" % (g, c))
+            nc.sync.dma_start(
+                out=x_raw[g, c][:],
+                in_=x_rows[
+                    g * K_PASS : (g + 1) * K_PASS, c * X_CHUNK : (c + 1) * X_CHUNK
+                ].rearrange("(p t) n -> p t n", t=PACK),
+            )
 
         def load_w(h):
             w_raw[h] = keep.tile([P, 2 * FEATURES], BF16, name="w_raw%d" % h)
@@ -63,13 +62,15 @@ def tile_gat_pa_kernel(tc, x, W1, b1, W2, b2, W3, b3, out):
                 out=w_raw[h][:], in_=weights[h].rearrange("(m r) k -> m (r k)", r=2)
             )
 
-        load_x(0)
+        load_x(0, 0)
+        load_w(0)
+        load_x(1, 0)
         for h in range(HEADS):
             nc.sync.dma_start(
                 out=bias_rows[0:1, h, :], in_=biases[h].rearrange("(o d) -> o d", o=1)
             )
-        load_w(0)
-        load_x(1)
+        load_x(0, 1)
+        load_x(1, 1)
         load_w(1)
         load_w(2)
 
@@ -79,39 +80,39 @@ def tile_gat_pa_kernel(tc, x, W1, b1, W2, b2, W3, b3, out):
         nc.vector.memset(ones[:], 1.0)
         warm = keep.tile([P, 1], F32, name="warm")
         nc.vector.memset(warm[:], 1.0)
-        nc.scalar.activation(out=warm[:], in_=warm[:], func=ACT.Sqrt)
+        nc.scalar.activation(out=warm[:], in_=warm[:], func=ACT.Abs_reciprocal_sqrt)
 
         bias_all = keep.tile([P, HEADS, DIM], F32, name="bias_all")
-        for h in range(HEADS):
-            bias_ps = acc_psum.tile([P, DIM], F32, tag="acc")
-            nc.tensor.matmul(
-                out=bias_ps[:], lhsT=ones[:], rhs=bias_rows[:, h, :], start=True, stop=True
-            )
-            nc.scalar.copy(out=bias_all[:, h, :], in_=bias_ps[:])
+
+        def spread_biases():
+            for h in range(HEADS):
+                bias_ps = acc_psum.tile([P, DIM], F32, tag="acc")
+                nc.tensor.matmul(
+                    out=bias_ps[:], lhsT=ones[:], rhs=bias_rows[:, h, :], start=True, stop=True
+                )
+                nc.scalar.copy(out=bias_all[:, h, :], in_=bias_ps[:])
 
         x_codes = keep.tile([P, PASSES, NODES], U32, name="x_codes", align_bytes=64)
         x_scales = keep.tile([P, PASSES, NODES], U8, name="x_scales", align_bytes=64)
         x_grouped = {}
 
-        def regroup_x(c):
-            for g in range(PASSES):
-                x_grouped[g, c] = keep.tile(
-                    [P, X_CHUNK, PACK], BF16, name="x_grouped%d_%d" % (g, c), align_bytes=64
-                )
-                dst = x_grouped[g, c][:].rearrange("p (c i) t -> p c t i", i=4)
-                src = x_raw[g, c][:].rearrange("p t (c i) -> p c t i", i=4)
-                cut = X_VECTOR_NODES // 4
-                nc.vector.tensor_copy(out=dst[:, :cut], in_=src[:, :cut])
-                nc.scalar.copy(out=dst[:, cut:], in_=src[:, cut:])
+        def regroup_x(g, c):
+            x_grouped[g, c] = keep.tile(
+                [P, X_CHUNK, PACK], BF16, name="x_grouped%d_%d" % (g, c), align_bytes=64
+            )
+            dst = x_grouped[g, c][:].rearrange("p (c i) t -> p c t i", i=4)
+            src = x_raw[g, c][:].rearrange("p t (c i) -> p c t i", i=4)
+            cut = X_VECTOR_NODES // 4
+            nc.vector.tensor_copy(out=dst[:, :cut], in_=src[:, :cut])
+            nc.scalar.copy(out=dst[:, cut:], in_=src[:, cut:])
 
-        def quantise_x(c):
+        def quantise_x(g, c):
             nodes = slice(c * X_CHUNK, (c + 1) * X_CHUNK)
-            for g in range(PASSES):
-                nc.vector.quantize_mx(
-                    out=x_codes[:, g, nodes].bitcast(FP8X4),
-                    scales=x_scales[:, g, nodes],
-                    in_=x_grouped[g, c][:].rearrange("p n t -> p (n t)"),
-                )
+            nc.vector.quantize_mx(
+                out=x_codes[:, g, nodes].bitcast(FP8X4),
+                scales=x_scales[:, g, nodes],
+                in_=x_grouped[g, c][:].rearrange("p n t -> p (n t)"),
+            )
 
         w_codes = keep.tile([P, HEADS, PASSES, DIM], U32, name="w_codes", align_bytes=64)
         w_scales = keep.tile([P, HEADS, PASSES, DIM], U8, name="w_scales", align_bytes=64)
@@ -184,13 +185,14 @@ def tile_gat_pa_kernel(tc, x, W1, b1, W2, b2, W3, b3, out):
                 )
 
         def invert_norms(j):
-            inv_sq = stats.tile([P, PAIR], F32, tag="inv_sq")
-            nc.vector.tensor_scalar(
-                out=inv_sq[:], in0=sumsq[j][:], scalar1=EPS * EPS, scalar2=None, op0=ALU.max
+            clamped = stats.tile([P, PAIR], F32, tag="clamped")
+            nc.gpsimd.tensor_scalar(
+                out=clamped[:], in0=sumsq[j][:], scalar1=EPS * EPS, scalar2=None, op0=ALU.max
             )
-            nc.vector.reciprocal(out=inv_sq[:], in_=inv_sq[:])
             inv_norm[j] = stats.tile([P, PAIR], F32, name="inv_norm", tag="inv_norm")
-            nc.scalar.activation(out=inv_norm[j][:], in_=inv_sq[:], func=ACT.Sqrt)
+            nc.scalar.activation(
+                out=inv_norm[j][:], in_=clamped[:], func=ACT.Abs_reciprocal_sqrt
+            )
 
         def scale_and_store(j):
             h, q = divmod(j, PAIRS_PER_HEAD)
@@ -216,11 +218,14 @@ def tile_gat_pa_kernel(tc, x, W1, b1, W2, b2, W3, b3, out):
                 in_=result[j][:],
             )
 
-        regroup_x(0)
-        quantise_x(0)
+        regroup_x(0, 0)
         transpose_w(0)
-        regroup_x(1)
+        quantise_x(0, 0)
+        regroup_x(1, 0)
+        spread_biases()
         quantise_w(0)
+        quantise_x(1, 0)
+        regroup_x(0, 1)
         for step in range(N_PAIRS + 3):
             if step < N_PAIRS:
                 project(step)
@@ -229,7 +234,9 @@ def tile_gat_pa_kernel(tc, x, W1, b1, W2, b2, W3, b3, out):
             if step >= 3:
                 scale_and_store(step - 3)
             if step == 0:
-                quantise_x(1)
+                regroup_x(1, 1)
+                quantise_x(0, 1)
+                quantise_x(1, 1)
             h, q = divmod(step, PAIRS_PER_HEAD)
             if h + 1 < HEADS and q == 1:
                 transpose_w(h + 1)

@@ -40,7 +40,7 @@ def tile_gat_pa_kernel(tc, x, W1, b1, W2, b2, W3, b3, out):
         name="stats", bufs=6
     ) as stats, tc.psum_pool(name="wt_psum", bufs=2) as wt_psum, tc.psum_pool(
         name="acc_psum", bufs=4
-    ) as acc_psum, tc.manual_schedule():
+    ) as acc_psum:
         bias_rows = keep.tile([P, HEADS, DIM], BF16, name="bias_rows")
         nc.vector.memset(bias_rows[:], 0.0)
 

@@ -23,9 +23,8 @@ FLOPS = 2 * NODES * FEATURES * HEADS * DIM
 X_CHUNK = 512
 X_CHUNKS = NODES // X_CHUNK
 X_VECTOR_NODES = 320
+TILES = X_CHUNK // P
 PAIR = 2
-PAIRS_PER_HEAD = NODES // (PAIR * P)
-N_PAIRS = HEADS * PAIRS_PER_HEAD
 
 
 def tile_gat_pa_kernel(tc, x, W1, b1, W2, b2, W3, b3, out):
@@ -35,15 +34,12 @@ def tile_gat_pa_kernel(tc, x, W1, b1, W2, b2, W3, b3, out):
     x_rows = x.rearrange("b f i j -> (b f) (i j)")
 
     with tc.tile_pool(name="keep", bufs=1) as keep, tc.tile_pool(
-        name="hidden_pool", bufs=6
-    ) as hidden_pool, tc.tile_pool(name="result_pool", bufs=8) as result_pool, tc.tile_pool(
-        name="stats", bufs=6
-    ) as stats, tc.psum_pool(name="wt_psum", bufs=2) as wt_psum, tc.psum_pool(
+        name="work", bufs=4
+    ) as work, tc.psum_pool(name="wt_psum", bufs=2) as wt_psum, tc.psum_pool(
         name="acc_psum", bufs=4
     ) as acc_psum:
         bias_rows = keep.tile([P, HEADS, DIM], BF16, name="bias_rows")
         nc.vector.memset(bias_rows[:], 0.0)
-
         x_raw = {}
         w_raw = {}
 
@@ -94,38 +90,28 @@ def tile_gat_pa_kernel(tc, x, W1, b1, W2, b2, W3, b3, out):
 
         x_codes = keep.tile([P, PASSES, NODES], U32, name="x_codes", align_bytes=64)
         x_scales = keep.tile([P, PASSES, NODES], U8, name="x_scales", align_bytes=64)
-        x_grouped = {}
 
-        def regroup_x(g, c):
-            x_grouped[g, c] = keep.tile(
+        def quantise_x(g, c):
+            grouped = keep.tile(
                 [P, X_CHUNK, PACK], BF16, name="x_grouped%d_%d" % (g, c), align_bytes=64
             )
-            dst = x_grouped[g, c][:].rearrange("p (c i) t -> p c t i", i=4)
+            dst = grouped[:].rearrange("p (c i) t -> p c t i", i=4)
             src = x_raw[g, c][:].rearrange("p t (c i) -> p c t i", i=4)
             cut = X_VECTOR_NODES // 4
             nc.vector.tensor_copy(out=dst[:, :cut], in_=src[:, :cut])
             nc.scalar.copy(out=dst[:, cut:], in_=src[:, cut:])
-
-        def quantise_x(g, c):
             nodes = slice(c * X_CHUNK, (c + 1) * X_CHUNK)
             nc.vector.quantize_mx(
                 out=x_codes[:, g, nodes].bitcast(FP8X4),
                 scales=x_scales[:, g, nodes],
-                in_=x_grouped[g, c][:].rearrange("p n t -> p (n t)"),
+                in_=grouped[:].rearrange("p n t -> p (n t)"),
             )
 
         w_codes = keep.tile([P, HEADS, PASSES, DIM], U32, name="w_codes", align_bytes=64)
         w_scales = keep.tile([P, HEADS, PASSES, DIM], U8, name="w_scales", align_bytes=64)
-        w_grouped = {}
 
-        def transpose_w(h):
+        def quantise_w(h):
             words = w_raw[h][:].bitcast(F32).rearrange("m (r w) -> m r w", r=2)
-            w_grouped[h] = keep.tile(
-                [P, PASSES * DIM * PACK], BF16, name="w_grouped%d" % h, align_bytes=64
-            )
-            grouped_words = w_grouped[h][:].bitcast(F32).rearrange(
-                "p (g m r u) -> p g m r u", g=PASSES, r=2, u=2
-            )
             for g in range(PASSES):
                 wt = wt_psum.tile([P, 2, 2, P], F32, tag="wt")
                 for r in range(2):
@@ -135,110 +121,91 @@ def tile_gat_pa_kernel(tc, x, W1, b1, W2, b2, W3, b3, out):
                             words[:, r, 256 * g + u : 256 * (g + 1) : 2],
                             ident[:],
                         )
-                nc.scalar.copy(
-                    out=grouped_words[:, g], in_=wt[:].rearrange("p r u m -> p m r u")
+                grouped = keep.tile(
+                    [P, DIM * PACK], BF16, name="w_grouped%d_%d" % (h, g), align_bytes=64
                 )
-
-        def quantise_w(h):
-            for g in range(PASSES):
+                nc.vector.tensor_copy(
+                    out=grouped[:].bitcast(F32).rearrange("p (m r u) -> p m r u", r=2, u=2),
+                    in_=wt[:].rearrange("p r u m -> p m r u"),
+                )
                 nc.vector.quantize_mx(
                     out=w_codes[:, h, g, :].bitcast(FP8X4),
                     scales=w_scales[:, h, g, :],
-                    in_=w_grouped[h][:, g * DIM * PACK : (g + 1) * DIM * PACK],
+                    in_=grouped[:],
                 )
 
-        hidden = {}
-        result = {}
-        sumsq = {}
-        inv_norm = {}
-
-        def project(j):
-            h, q = divmod(j, PAIRS_PER_HEAD)
-            acc = acc_psum.tile([P, PAIR, DIM], F32, tag="acc")
-            for m in range(PAIR):
-                nodes = slice((q * PAIR + m) * P, (q * PAIR + m + 1) * P)
-                for g in range(PASSES):
-                    nc.tensor.matmul_mx(
-                        out=acc[:, m, :],
-                        lhsT=x_codes[:, g, nodes].bitcast(FP8X4),
-                        lhsT_scale=x_scales[:, g, nodes],
-                        rhs=w_codes[:, h, g, :].bitcast(FP8X4),
-                        rhs_scale=w_scales[:, h, g, :],
-                        start=(g == 0),
-                        stop=(g == PASSES - 1),
+        def project(h, c):
+            hidden = work.tile([P, TILES, DIM], F32, tag="hidden")
+            result = work.tile([P, TILES, DIM], F32, tag="result")
+            sumsq = work.tile([P, TILES], F32, tag="sumsq")
+            for first in range(0, TILES, PAIR):
+                acc = acc_psum.tile([P, PAIR, DIM], F32, tag="acc")
+                for m in range(PAIR):
+                    start_node = c * X_CHUNK + (first + m) * P
+                    nodes = slice(start_node, start_node + P)
+                    for g in range(PASSES):
+                        nc.tensor.matmul_mx(
+                            out=acc[:, m, :],
+                            lhsT=x_codes[:, g, nodes].bitcast(FP8X4),
+                            lhsT_scale=x_scales[:, g, nodes],
+                            rhs=w_codes[:, h, g, :].bitcast(FP8X4),
+                            rhs_scale=w_scales[:, h, g, :],
+                            start=(g == 0),
+                            stop=(g == PASSES - 1),
+                        )
+                nc.vector.tensor_tensor(
+                    out=hidden[:, first : first + PAIR, :],
+                    in0=acc[:],
+                    in1=bias_all[:, h : h + 1, :].to_broadcast([P, PAIR, DIM]),
+                    op=ALU.add,
+                )
+                for t in range(first, first + PAIR):
+                    nc.scalar.activation(
+                        out=result[:, t, :],
+                        in_=hidden[:, t, :],
+                        func=ACT.Square,
+                        accum_out=sumsq[:, t : t + 1],
                     )
-            hidden[j] = hidden_pool.tile([P, PAIR, DIM], F32, name="hidden", tag="hidden")
-            nc.vector.tensor_tensor(
-                out=hidden[j][:],
-                in0=acc[:],
-                in1=bias_all[:, h : h + 1, :].to_broadcast([P, PAIR, DIM]),
-                op=ALU.add,
+            clamped = work.tile([P, TILES], F32, tag="clamped")
+            nc.gpsimd.tensor_scalar(
+                out=clamped[:], in0=sumsq[:], scalar1=EPS * EPS, scalar2=None, op0=ALU.max
             )
-            result[j] = result_pool.tile([P, PAIR, DIM], F32, name="result", tag="result")
-            sumsq[j] = stats.tile([P, PAIR], F32, name="sumsq", tag="sumsq")
-            for m in range(PAIR):
-                nc.scalar.activation(
-                    out=result[j][:, m, :],
-                    in_=hidden[j][:, m, :],
-                    func=ACT.Square,
-                    accum_out=sumsq[j][:, m : m + 1],
+            inv_norm = work.tile([P, TILES], F32, tag="inv_norm")
+            nc.scalar.activation(out=inv_norm[:], in_=clamped[:], func=ACT.Abs_reciprocal_sqrt)
+            for t in range(TILES):
+                if t % 2 == 0:
+                    nc.gpsimd.tensor_scalar(
+                        out=result[:, t, :],
+                        in0=hidden[:, t, :],
+                        scalar1=inv_norm[:, t : t + 1],
+                        scalar2=0.0,
+                        op0=ALU.mult,
+                        op1=ALU.add,
+                    )
+                else:
+                    nc.scalar.activation(
+                        out=result[:, t, :],
+                        in_=hidden[:, t, :],
+                        func=ACT.Copy,
+                        scale=inv_norm[:, t : t + 1],
+                    )
+            for first in range(0, TILES, PAIR):
+                start_node = c * X_CHUNK + first * P
+                nc.sync.dma_start(
+                    out=out[h, start_node : start_node + PAIR * P, :].rearrange(
+                        "(m p) d -> p m d", p=P
+                    ),
+                    in_=result[:, first : first + PAIR, :],
                 )
 
-        def invert_norms(j):
-            clamped = stats.tile([P, PAIR], F32, tag="clamped")
-            nc.gpsimd.tensor_scalar(
-                out=clamped[:], in0=sumsq[j][:], scalar1=EPS * EPS, scalar2=None, op0=ALU.max
-            )
-            inv_norm[j] = stats.tile([P, PAIR], F32, name="inv_norm", tag="inv_norm")
-            nc.scalar.activation(
-                out=inv_norm[j][:], in_=clamped[:], func=ACT.Abs_reciprocal_sqrt
-            )
-
-        def scale_and_store(j):
-            h, q = divmod(j, PAIRS_PER_HEAD)
-            nc.gpsimd.tensor_scalar(
-                out=result[j][:, 0, :],
-                in0=hidden[j][:, 0, :],
-                scalar1=inv_norm[j][:, 0:1],
-                scalar2=0.0,
-                op0=ALU.mult,
-                op1=ALU.add,
-            )
-            nc.vector.tensor_scalar(
-                out=result[j][:, 1, :],
-                in0=hidden[j][:, 1, :],
-                scalar1=inv_norm[j][:, 1:2],
-                scalar2=None,
-                op0=ALU.mult,
-            )
-            nc.sync.dma_start(
-                out=out[h, q * PAIR * P : (q + 1) * PAIR * P, :].rearrange(
-                    "(m p) d -> p m d", p=P
-                ),
-                in_=result[j][:],
-            )
-
-        regroup_x(0, 0)
-        transpose_w(0)
         quantise_x(0, 0)
-        regroup_x(1, 0)
-        spread_biases()
         quantise_w(0)
         quantise_x(1, 0)
-        regroup_x(0, 1)
-        for step in range(N_PAIRS + 3):
-            if step < N_PAIRS:
-                project(step)
-            if 1 <= step <= N_PAIRS:
-                invert_norms(step - 1)
-            if step >= 3:
-                scale_and_store(step - 3)
-            if step == 0:
-                regroup_x(1, 1)
-                quantise_x(0, 1)
-                quantise_x(1, 1)
-            h, q = divmod(step, PAIRS_PER_HEAD)
-            if h + 1 < HEADS and q == 1:
-                transpose_w(h + 1)
-            if h + 1 < HEADS and q == 2:
+        spread_biases()
+        quantise_x(0, 1)
+        quantise_x(1, 1)
+        for h in range(HEADS):
+            if h + 1 < HEADS:
                 quantise_w(h + 1)
+            for c in range(X_CHUNKS):
+                project(h, c)

@@ -23,8 +23,9 @@ FLOPS = 2 * NODES * FEATURES * HEADS * DIM
 X_CHUNK = 512
 X_CHUNKS = NODES // X_CHUNK
 X_VECTOR_NODES = 320
-TILES = X_CHUNK // P
 PAIR = 2
+PAIRS_PER_CHUNK = X_CHUNK // (PAIR * P)
+N_PAIRS = X_CHUNKS * HEADS * PAIRS_PER_CHUNK
 
 
 def tile_gat_pa_kernel(tc, x, W1, b1, W2, b2, W3, b3, out):
@@ -34,12 +35,15 @@ def tile_gat_pa_kernel(tc, x, W1, b1, W2, b2, W3, b3, out):
     x_rows = x.rearrange("b f i j -> (b f) (i j)")
 
     with tc.tile_pool(name="keep", bufs=1) as keep, tc.tile_pool(
-        name="work", bufs=4
-    ) as work, tc.psum_pool(name="wt_psum", bufs=2) as wt_psum, tc.psum_pool(
+        name="hidden_pool", bufs=6
+    ) as hidden_pool, tc.tile_pool(name="result_pool", bufs=8) as result_pool, tc.tile_pool(
+        name="stats", bufs=6
+    ) as stats, tc.psum_pool(name="wt_psum", bufs=2) as wt_psum, tc.psum_pool(
         name="acc_psum", bufs=4
     ) as acc_psum:
         bias_rows = keep.tile([P, HEADS, DIM], BF16, name="bias_rows")
         nc.vector.memset(bias_rows[:], 0.0)
+
         x_raw = {}
         w_raw = {}
 
@@ -65,10 +69,10 @@ def tile_gat_pa_kernel(tc, x, W1, b1, W2, b2, W3, b3, out):
             nc.sync.dma_start(
                 out=bias_rows[0:1, h, :], in_=biases[h].rearrange("(o d) -> o d", o=1)
             )
-        load_x(0, 1)
-        load_x(1, 1)
         load_w(1)
         load_w(2)
+        load_x(0, 1)
+        load_x(1, 1)
 
         ident = keep.tile([P, P], F32, name="ident")
         make_identity(nc, ident[:])
@@ -90,28 +94,38 @@ def tile_gat_pa_kernel(tc, x, W1, b1, W2, b2, W3, b3, out):
 
         x_codes = keep.tile([P, PASSES, NODES], U32, name="x_codes", align_bytes=64)
         x_scales = keep.tile([P, PASSES, NODES], U8, name="x_scales", align_bytes=64)
+        x_grouped = {}
 
-        def quantise_x(g, c):
-            grouped = keep.tile(
+        def regroup_x(g, c):
+            x_grouped[g, c] = keep.tile(
                 [P, X_CHUNK, PACK], BF16, name="x_grouped%d_%d" % (g, c), align_bytes=64
             )
-            dst = grouped[:].rearrange("p (c i) t -> p c t i", i=4)
+            dst = x_grouped[g, c][:].rearrange("p (c i) t -> p c t i", i=4)
             src = x_raw[g, c][:].rearrange("p t (c i) -> p c t i", i=4)
             cut = X_VECTOR_NODES // 4
             nc.vector.tensor_copy(out=dst[:, :cut], in_=src[:, :cut])
             nc.scalar.copy(out=dst[:, cut:], in_=src[:, cut:])
+
+        def quantise_x(g, c):
             nodes = slice(c * X_CHUNK, (c + 1) * X_CHUNK)
             nc.vector.quantize_mx(
                 out=x_codes[:, g, nodes].bitcast(FP8X4),
                 scales=x_scales[:, g, nodes],
-                in_=grouped[:].rearrange("p n t -> p (n t)"),
+                in_=x_grouped[g, c][:].rearrange("p n t -> p (n t)"),
             )
 
         w_codes = keep.tile([P, HEADS, PASSES, DIM], U32, name="w_codes", align_bytes=64)
         w_scales = keep.tile([P, HEADS, PASSES, DIM], U8, name="w_scales", align_bytes=64)
+        w_grouped = {}
 
-        def quantise_w(h):
+        def transpose_w(h):
             words = w_raw[h][:].bitcast(F32).rearrange("m (r w) -> m r w", r=2)
+            w_grouped[h] = keep.tile(
+                [P, PASSES * DIM * PACK], BF16, name="w_grouped%d" % h, align_bytes=64
+            )
+            grouped_words = w_grouped[h][:].bitcast(F32).rearrange(
+                "p (g m r u) -> p g m r u", g=PASSES, r=2, u=2
+            )
             for g in range(PASSES):
                 wt = wt_psum.tile([P, 2, 2, P], F32, tag="wt")
                 for r in range(2):
@@ -121,91 +135,113 @@ def tile_gat_pa_kernel(tc, x, W1, b1, W2, b2, W3, b3, out):
                             words[:, r, 256 * g + u : 256 * (g + 1) : 2],
                             ident[:],
                         )
-                grouped = keep.tile(
-                    [P, DIM * PACK], BF16, name="w_grouped%d_%d" % (h, g), align_bytes=64
+                nc.scalar.copy(
+                    out=grouped_words[:, g], in_=wt[:].rearrange("p r u m -> p m r u")
                 )
-                nc.vector.tensor_copy(
-                    out=grouped[:].bitcast(F32).rearrange("p (m r u) -> p m r u", r=2, u=2),
-                    in_=wt[:].rearrange("p r u m -> p m r u"),
-                )
+
+        def quantise_w(h):
+            for g in range(PASSES):
                 nc.vector.quantize_mx(
                     out=w_codes[:, h, g, :].bitcast(FP8X4),
                     scales=w_scales[:, h, g, :],
-                    in_=grouped[:],
+                    in_=w_grouped[h][:, g * DIM * PACK : (g + 1) * DIM * PACK],
                 )
 
-        def project(h, c):
-            hidden = work.tile([P, TILES, DIM], F32, tag="hidden")
-            result = work.tile([P, TILES, DIM], F32, tag="result")
-            sumsq = work.tile([P, TILES], F32, tag="sumsq")
-            for first in range(0, TILES, PAIR):
-                acc = acc_psum.tile([P, PAIR, DIM], F32, tag="acc")
-                for m in range(PAIR):
-                    start_node = c * X_CHUNK + (first + m) * P
-                    nodes = slice(start_node, start_node + P)
-                    for g in range(PASSES):
-                        nc.tensor.matmul_mx(
-                            out=acc[:, m, :],
-                            lhsT=x_codes[:, g, nodes].bitcast(FP8X4),
-                            lhsT_scale=x_scales[:, g, nodes],
-                            rhs=w_codes[:, h, g, :].bitcast(FP8X4),
-                            rhs_scale=w_scales[:, h, g, :],
-                            start=(g == 0),
-                            stop=(g == PASSES - 1),
-                        )
-                nc.vector.tensor_tensor(
-                    out=hidden[:, first : first + PAIR, :],
-                    in0=acc[:],
-                    in1=bias_all[:, h : h + 1, :].to_broadcast([P, PAIR, DIM]),
-                    op=ALU.add,
-                )
-                for t in range(first, first + PAIR):
-                    nc.scalar.activation(
-                        out=result[:, t, :],
-                        in_=hidden[:, t, :],
-                        func=ACT.Square,
-                        accum_out=sumsq[:, t : t + 1],
+        hidden = {}
+        result = {}
+        sumsq = {}
+        inv_norm = {}
+
+        def head_and_first_node(j):
+            c, rest = divmod(j, HEADS * PAIRS_PER_CHUNK)
+            h, i = divmod(rest, PAIRS_PER_CHUNK)
+            return h, c * X_CHUNK + i * PAIR * P
+
+        def project(j):
+            h, first_node = head_and_first_node(j)
+            acc = acc_psum.tile([P, PAIR, DIM], F32, tag="acc")
+            for m in range(PAIR):
+                nodes = slice(first_node + m * P, first_node + (m + 1) * P)
+                for g in range(PASSES):
+                    nc.tensor.matmul_mx(
+                        out=acc[:, m, :],
+                        lhsT=x_codes[:, g, nodes].bitcast(FP8X4),
+                        lhsT_scale=x_scales[:, g, nodes],
+                        rhs=w_codes[:, h, g, :].bitcast(FP8X4),
+                        rhs_scale=w_scales[:, h, g, :],
+                        start=(g == 0),
+                        stop=(g == PASSES - 1),
                     )
-            clamped = work.tile([P, TILES], F32, tag="clamped")
-            nc.gpsimd.tensor_scalar(
-                out=clamped[:], in0=sumsq[:], scalar1=EPS * EPS, scalar2=None, op0=ALU.max
+            hidden[j] = hidden_pool.tile([P, PAIR, DIM], F32, name="hidden", tag="hidden")
+            nc.vector.tensor_tensor(
+                out=hidden[j][:],
+                in0=acc[:],
+                in1=bias_all[:, h : h + 1, :].to_broadcast([P, PAIR, DIM]),
+                op=ALU.add,
             )
-            inv_norm = work.tile([P, TILES], F32, tag="inv_norm")
-            nc.scalar.activation(out=inv_norm[:], in_=clamped[:], func=ACT.Abs_reciprocal_sqrt)
-            for t in range(TILES):
-                if t % 2 == 0:
-                    nc.gpsimd.tensor_scalar(
-                        out=result[:, t, :],
-                        in0=hidden[:, t, :],
-                        scalar1=inv_norm[:, t : t + 1],
-                        scalar2=0.0,
-                        op0=ALU.mult,
-                        op1=ALU.add,
-                    )
-                else:
-                    nc.scalar.activation(
-                        out=result[:, t, :],
-                        in_=hidden[:, t, :],
-                        func=ACT.Copy,
-                        scale=inv_norm[:, t : t + 1],
-                    )
-            for first in range(0, TILES, PAIR):
-                start_node = c * X_CHUNK + first * P
-                nc.sync.dma_start(
-                    out=out[h, start_node : start_node + PAIR * P, :].rearrange(
-                        "(m p) d -> p m d", p=P
-                    ),
-                    in_=result[:, first : first + PAIR, :],
+            result[j] = result_pool.tile([P, PAIR, DIM], F32, name="result", tag="result")
+            sumsq[j] = stats.tile([P, PAIR], F32, name="sumsq", tag="sumsq")
+            for m in range(PAIR):
+                nc.scalar.activation(
+                    out=result[j][:, m, :],
+                    in_=hidden[j][:, m, :],
+                    func=ACT.Square,
+                    accum_out=sumsq[j][:, m : m + 1],
                 )
 
+        def invert_norms(j):
+            clamped = stats.tile([P, PAIR], F32, tag="clamped")
+            nc.gpsimd.tensor_scalar(
+                out=clamped[:], in0=sumsq[j][:], scalar1=EPS * EPS, scalar2=None, op0=ALU.max
+            )
+            inv_norm[j] = stats.tile([P, PAIR], F32, name="inv_norm", tag="inv_norm")
+            nc.scalar.activation(
+                out=inv_norm[j][:], in_=clamped[:], func=ACT.Abs_reciprocal_sqrt
+            )
+
+        def scale_and_store(j):
+            h, first_node = head_and_first_node(j)
+            nc.gpsimd.tensor_scalar(
+                out=result[j][:, 0, :],
+                in0=hidden[j][:, 0, :],
+                scalar1=inv_norm[j][:, 0:1],
+                scalar2=0.0,
+                op0=ALU.mult,
+                op1=ALU.add,
+            )
+            nc.vector.tensor_scalar(
+                out=result[j][:, 1, :],
+                in0=hidden[j][:, 1, :],
+                scalar1=inv_norm[j][:, 1:2],
+                scalar2=None,
+                op0=ALU.mult,
+            )
+            nc.sync.dma_start(
+                out=out[h, first_node : first_node + PAIR * P, :].rearrange(
+                    "(m p) d -> p m d", p=P
+                ),
+                in_=result[j][:],
+            )
+
+        regroup_x(0, 0)
+        transpose_w(0)
         quantise_x(0, 0)
+        regroup_x(1, 0)
+        spread_biases()
         quantise_w(0)
         quantise_x(1, 0)
-        spread_biases()
-        quantise_x(0, 1)
-        quantise_x(1, 1)
-        for h in range(HEADS):
-            if h + 1 < HEADS:
-                quantise_w(h + 1)
-            for c in range(X_CHUNKS):
-                project(h, c)
+        for step in range(N_PAIRS + 3):
+            if step < N_PAIRS:
+                project(step)
+            if 1 <= step <= N_PAIRS:
+                invert_norms(step - 1)
+            if step >= 3:
+                scale_and_store(step - 3)
+            if step == 0 or step == 1:
+                transpose_w(step + 1)
+                quantise_w(step + 1)
+            if step == 2:
+                for g in range(PASSES):
+                    regroup_x(g, 1)
+                for g in range(PASSES):
+                    quantise_x(g, 1)

@@ -1,3 +1,5 @@
+from contextlib import ExitStack
+
 import concourse.mybir as mybir
 from concourse.masks import make_identity
 
@@ -26,6 +28,7 @@ X_VECTOR_NODES = 320
 PAIR = 2
 PAIRS_PER_CHUNK = X_CHUNK // (PAIR * P)
 N_PAIRS = X_CHUNKS * HEADS * PAIRS_PER_CHUNK
+SCALE_AFTER = 3
 
 
 def tile_gat_pa_kernel(tc, x, W1, b1, W2, b2, W3, b3, out):
@@ -40,9 +43,18 @@ def tile_gat_pa_kernel(tc, x, W1, b1, W2, b2, W3, b3, out):
         name="stats", bufs=6
     ) as stats, tc.psum_pool(name="wt_psum", bufs=2) as wt_psum, tc.psum_pool(
         name="acc_psum", bufs=4
-    ) as acc_psum:
+    ) as acc_psum, ExitStack() as ctx:
+        ctx.enter_context(tc.manual_schedule())
+
         bias_rows = keep.tile([P, HEADS, DIM], BF16, name="bias_rows")
         nc.vector.memset(bias_rows[:], 0.0)
+        ident = keep.tile([P, P], F32, name="ident")
+        make_identity(nc, ident[:])
+        ones = keep.tile([P, P], BF16, name="ones")
+        nc.vector.memset(ones[:], 1.0)
+        warm = keep.tile([P, 1], F32, name="warm")
+        nc.vector.memset(warm[:], 1.0)
+        nc.scalar.activation(out=warm[:], in_=warm[:], func=ACT.Abs_reciprocal_sqrt)
 
         x_raw = {}
         w_raw = {}
@@ -74,36 +86,39 @@ def tile_gat_pa_kernel(tc, x, W1, b1, W2, b2, W3, b3, out):
         load_x(0, 1)
         load_x(1, 1)
 
-        ident = keep.tile([P, P], F32, name="ident")
-        make_identity(nc, ident[:])
-        ones = keep.tile([P, P], BF16, name="ones")
-        nc.vector.memset(ones[:], 1.0)
-        warm = keep.tile([P, 1], F32, name="warm")
-        nc.vector.memset(warm[:], 1.0)
-        nc.scalar.activation(out=warm[:], in_=warm[:], func=ACT.Abs_reciprocal_sqrt)
-
         bias_all = keep.tile([P, HEADS, DIM], F32, name="bias_all")
+        bias_ps = {}
 
-        def spread_biases():
-            for h in range(HEADS):
-                bias_ps = acc_psum.tile([P, DIM], F32, tag="acc")
-                nc.tensor.matmul(
-                    out=bias_ps[:], lhsT=ones[:], rhs=bias_rows[:, h, :], start=True, stop=True
-                )
-                nc.scalar.copy(out=bias_all[:, h, :], in_=bias_ps[:])
+        def bias_matmul(h):
+            bias_ps[h] = acc_psum.tile([P, DIM], F32, name="bias_ps", tag="acc")
+            nc.tensor.matmul(
+                out=bias_ps[h][:], lhsT=ones[:], rhs=bias_rows[:, h, :], start=True, stop=True
+            )
+
+        def bias_copy(h):
+            nc.scalar.copy(out=bias_all[:, h, :], in_=bias_ps[h][:])
 
         x_codes = keep.tile([P, PASSES, NODES], U32, name="x_codes", align_bytes=64)
         x_scales = keep.tile([P, PASSES, NODES], U8, name="x_scales", align_bytes=64)
         x_grouped = {}
+        quantised = set()
+        cut = X_VECTOR_NODES // 4
 
-        def regroup_x(g, c):
-            x_grouped[g, c] = keep.tile(
-                [P, X_CHUNK, PACK], BF16, name="x_grouped%d_%d" % (g, c), align_bytes=64
-            )
+        def grouped_views(g, c):
+            if (g, c) not in x_grouped:
+                x_grouped[g, c] = keep.tile(
+                    [P, X_CHUNK, PACK], BF16, name="x_grouped%d_%d" % (g, c), align_bytes=64
+                )
             dst = x_grouped[g, c][:].rearrange("p (c i) t -> p c t i", i=4)
             src = x_raw[g, c][:].rearrange("p t (c i) -> p c t i", i=4)
-            cut = X_VECTOR_NODES // 4
+            return dst, src
+
+        def regroup_x_vector(g, c):
+            dst, src = grouped_views(g, c)
             nc.vector.tensor_copy(out=dst[:, :cut], in_=src[:, :cut])
+
+        def regroup_x_scalar(g, c):
+            dst, src = grouped_views(g, c)
             nc.scalar.copy(out=dst[:, cut:], in_=src[:, cut:])
 
         def quantise_x(g, c):
@@ -113,58 +128,70 @@ def tile_gat_pa_kernel(tc, x, W1, b1, W2, b2, W3, b3, out):
                 scales=x_scales[:, g, nodes],
                 in_=x_grouped[g, c][:].rearrange("p n t -> p (n t)"),
             )
+            quantised.add(("x", g, c))
 
         w_codes = keep.tile([P, HEADS, PASSES, DIM], U32, name="w_codes", align_bytes=64)
         w_scales = keep.tile([P, HEADS, PASSES, DIM], U8, name="w_scales", align_bytes=64)
         w_grouped = {}
+        w_turned = {}
 
-        def transpose_w(h):
+        def transpose_w(h, g):
             words = w_raw[h][:].bitcast(F32).rearrange("m (r w) -> m r w", r=2)
-            w_grouped[h] = keep.tile(
-                [P, PASSES * DIM * PACK], BF16, name="w_grouped%d" % h, align_bytes=64
-            )
+            w_turned[h, g] = wt_psum.tile([P, 2, 2, P], F32, name="wt", tag="wt")
+            for r in range(2):
+                for u in range(2):
+                    nc.tensor.transpose(
+                        w_turned[h, g][:, r, u, :],
+                        words[:, r, 256 * g + u : 256 * (g + 1) : 2],
+                        ident[:],
+                    )
+
+        def empty_w(h, g):
+            if h not in w_grouped:
+                w_grouped[h] = keep.tile(
+                    [P, PASSES * DIM * PACK], BF16, name="w_grouped%d" % h, align_bytes=64
+                )
             grouped_words = w_grouped[h][:].bitcast(F32).rearrange(
                 "p (g m r u) -> p g m r u", g=PASSES, r=2, u=2
             )
-            for g in range(PASSES):
-                wt = wt_psum.tile([P, 2, 2, P], F32, tag="wt")
-                for r in range(2):
-                    for u in range(2):
-                        nc.tensor.transpose(
-                            wt[:, r, u, :],
-                            words[:, r, 256 * g + u : 256 * (g + 1) : 2],
-                            ident[:],
-                        )
-                nc.scalar.copy(
-                    out=grouped_words[:, g], in_=wt[:].rearrange("p r u m -> p m r u")
-                )
+            nc.scalar.copy(
+                out=grouped_words[:, g], in_=w_turned[h, g][:].rearrange("p r u m -> p m r u")
+            )
 
-        def quantise_w(h):
-            for g in range(PASSES):
-                nc.vector.quantize_mx(
-                    out=w_codes[:, h, g, :].bitcast(FP8X4),
-                    scales=w_scales[:, h, g, :],
-                    in_=w_grouped[h][:, g * DIM * PACK : (g + 1) * DIM * PACK],
-                )
+        def quantise_w(h, g):
+            nc.vector.quantize_mx(
+                out=w_codes[:, h, g, :].bitcast(FP8X4),
+                scales=w_scales[:, h, g, :],
+                in_=w_grouped[h][:, g * DIM * PACK : (g + 1) * DIM * PACK],
+            )
+            quantised.add(("w", h, g))
 
+        acc = {}
         hidden = {}
         result = {}
         sumsq = {}
+        clamped = {}
         inv_norm = {}
 
-        def head_and_first_node(j):
+        def place(j):
             c, rest = divmod(j, HEADS * PAIRS_PER_CHUNK)
             h, i = divmod(rest, PAIRS_PER_CHUNK)
-            return h, c * X_CHUNK + i * PAIR * P
+            return c, h, c * X_CHUNK + i * PAIR * P
 
-        def project(j):
-            h, first_node = head_and_first_node(j)
-            acc = acc_psum.tile([P, PAIR, DIM], F32, tag="acc")
+        def matmuls(j):
+            c, h, first_node = place(j)
+            if j >= N_PAIRS or j in acc:
+                return
+            if not all(
+                ("x", g, c) in quantised and ("w", h, g) in quantised for g in range(PASSES)
+            ):
+                return
+            acc[j] = acc_psum.tile([P, PAIR, DIM], F32, name="acc", tag="acc")
             for m in range(PAIR):
                 nodes = slice(first_node + m * P, first_node + (m + 1) * P)
                 for g in range(PASSES):
                     nc.tensor.matmul_mx(
-                        out=acc[:, m, :],
+                        out=acc[j][:, m, :],
                         lhsT=x_codes[:, g, nodes].bitcast(FP8X4),
                         lhsT_scale=x_scales[:, g, nodes],
                         rhs=w_codes[:, h, g, :].bitcast(FP8X4),
@@ -172,13 +199,18 @@ def tile_gat_pa_kernel(tc, x, W1, b1, W2, b2, W3, b3, out):
                         start=(g == 0),
                         stop=(g == PASSES - 1),
                     )
+
+        def add_bias(j):
+            c, h, first_node = place(j)
             hidden[j] = hidden_pool.tile([P, PAIR, DIM], F32, name="hidden", tag="hidden")
             nc.vector.tensor_tensor(
                 out=hidden[j][:],
-                in0=acc[:],
+                in0=acc[j][:],
                 in1=bias_all[:, h : h + 1, :].to_broadcast([P, PAIR, DIM]),
                 op=ALU.add,
             )
+
+        def squares(j):
             result[j] = result_pool.tile([P, PAIR, DIM], F32, name="result", tag="result")
             sumsq[j] = stats.tile([P, PAIR], F32, name="sumsq", tag="sumsq")
             for m in range(PAIR):
@@ -190,25 +222,34 @@ def tile_gat_pa_kernel(tc, x, W1, b1, W2, b2, W3, b3, out):
                 )
 
         def invert_norms(j):
-            clamped = stats.tile([P, PAIR], F32, tag="clamped")
+            clamped[j] = stats.tile([P, PAIR], F32, name="clamped", tag="clamped")
             nc.gpsimd.tensor_scalar(
-                out=clamped[:], in0=sumsq[j][:], scalar1=EPS * EPS, scalar2=None, op0=ALU.max
+                out=clamped[j][:], in0=sumsq[j][:], scalar1=EPS * EPS, scalar2=None, op0=ALU.max
             )
             inv_norm[j] = stats.tile([P, PAIR], F32, name="inv_norm", tag="inv_norm")
             nc.scalar.activation(
-                out=inv_norm[j][:], in_=clamped[:], func=ACT.Abs_reciprocal_sqrt
+                out=inv_norm[j][:], in_=clamped[j][:], func=ACT.Abs_reciprocal_sqrt
             )
 
         def scale_and_store(j):
-            h, first_node = head_and_first_node(j)
-            nc.gpsimd.tensor_scalar(
-                out=result[j][:, 0, :],
-                in0=hidden[j][:, 0, :],
-                scalar1=inv_norm[j][:, 0:1],
-                scalar2=0.0,
-                op0=ALU.mult,
-                op1=ALU.add,
-            )
+            c, h, first_node = place(j)
+            if j == N_PAIRS - 1:
+                nc.vector.tensor_scalar(
+                    out=result[j][:, 0, :],
+                    in0=hidden[j][:, 0, :],
+                    scalar1=inv_norm[j][:, 0:1],
+                    scalar2=None,
+                    op0=ALU.mult,
+                )
+            else:
+                nc.gpsimd.tensor_scalar(
+                    out=result[j][:, 0, :],
+                    in0=hidden[j][:, 0, :],
+                    scalar1=inv_norm[j][:, 0:1],
+                    scalar2=0.0,
+                    op0=ALU.mult,
+                    op1=ALU.add,
+                )
             nc.vector.tensor_scalar(
                 out=result[j][:, 1, :],
                 in0=hidden[j][:, 1, :],
@@ -223,25 +264,55 @@ def tile_gat_pa_kernel(tc, x, W1, b1, W2, b2, W3, b3, out):
                 in_=result[j][:],
             )
 
-        regroup_x(0, 0)
-        transpose_w(0)
+        regroup_x_vector(0, 0)
+        regroup_x_scalar(0, 0)
+        transpose_w(0, 0)
+        transpose_w(0, 1)
+        empty_w(0, 0)
         quantise_x(0, 0)
-        regroup_x(1, 0)
-        spread_biases()
-        quantise_w(0)
+        regroup_x_vector(1, 0)
+        regroup_x_scalar(1, 0)
+        empty_w(0, 1)
+        quantise_w(0, 0)
+        for h in range(HEADS):
+            bias_matmul(h)
+        transpose_w(1, 0)
+        transpose_w(1, 1)
+        bias_copy(0)
         quantise_x(1, 0)
-        for step in range(N_PAIRS + 3):
+        quantise_w(0, 1)
+        empty_w(1, 0)
+        empty_w(1, 1)
+        bias_copy(1)
+        bias_copy(2)
+        quantise_w(1, 0)
+
+        for step in range(N_PAIRS + SCALE_AFTER):
+            if step == 3:
+                quantise_w(2, 0)
+                quantise_w(2, 1)
+            matmuls(step)
+            if step == 0:
+                transpose_w(2, 0)
+                transpose_w(2, 1)
             if step < N_PAIRS:
-                project(step)
+                add_bias(step)
+                squares(step)
             if 1 <= step <= N_PAIRS:
                 invert_norms(step - 1)
-            if step >= 3:
-                scale_and_store(step - 3)
-            if step == 0 or step == 1:
-                transpose_w(step + 1)
-                quantise_w(step + 1)
+            if step == 0:
+                empty_w(2, 0)
+                empty_w(2, 1)
+            if step == 1 or step == 2:
+                regroup_x_scalar(step - 1, 1)
+            if step >= SCALE_AFTER:
+                scale_and_store(step - SCALE_AFTER)
+            if step == 0:
+                quantise_w(1, 1)
+                regroup_x_vector(0, 1)
             if step == 2:
-                for g in range(PASSES):
-                    regroup_x(g, 1)
-                for g in range(PASSES):
-                    quantise_x(g, 1)
+                regroup_x_vector(1, 1)
+            if step == 3 or step == 4:
+                quantise_x(step - 3, 1)
+            matmuls(step + 1)
+            matmuls(step + 2)

@@ -29,6 +29,7 @@ PAIR = 2
 PAIRS_PER_CHUNK = X_CHUNK // (PAIR * P)
 N_PAIRS = X_CHUNKS * HEADS * PAIRS_PER_CHUNK
 SCALE_AFTER = 3
+VECTOR_ALONE_FROM = 7
 
 
 def tile_gat_pa_kernel(tc, x, W1, b1, W2, b2, W3, b3, out):
@@ -173,21 +174,28 @@ def tile_gat_pa_kernel(tc, x, W1, b1, W2, b2, W3, b3, out):
         clamped = {}
         inv_norm = {}
 
-        def place(j):
+        groups = []
+        for j in range(N_PAIRS):
             c, rest = divmod(j, HEADS * PAIRS_PER_CHUNK)
             h, i = divmod(rest, PAIRS_PER_CHUNK)
-            return c, h, c * X_CHUNK + i * PAIR * P
+            first_node = c * X_CHUNK + i * PAIR * P
+            if j < N_PAIRS - 1:
+                groups.append((c, h, first_node, PAIR))
+            else:
+                for m in range(PAIR):
+                    groups.append((c, h, first_node + m * P, 1))
+        n_groups = len(groups)
 
         def matmuls(j):
-            c, h, first_node = place(j)
-            if j >= N_PAIRS or j in acc:
+            if j >= n_groups or j in acc:
                 return
+            c, h, first_node, tiles = groups[j]
             if not all(
                 ("x", g, c) in quantised and ("w", h, g) in quantised for g in range(PASSES)
             ):
                 return
             acc[j] = acc_psum.tile([P, PAIR, DIM], F32, name="acc", tag="acc")
-            for m in range(PAIR):
+            for m in range(tiles):
                 nodes = slice(first_node + m * P, first_node + (m + 1) * P)
                 for g in range(PASSES):
                     nc.tensor.matmul_mx(
@@ -201,19 +209,19 @@ def tile_gat_pa_kernel(tc, x, W1, b1, W2, b2, W3, b3, out):
                     )
 
         def add_bias(j):
-            c, h, first_node = place(j)
+            c, h, first_node, tiles = groups[j]
             hidden[j] = hidden_pool.tile([P, PAIR, DIM], F32, name="hidden", tag="hidden")
             nc.vector.tensor_tensor(
-                out=hidden[j][:],
-                in0=acc[j][:],
-                in1=bias_all[:, h : h + 1, :].to_broadcast([P, PAIR, DIM]),
+                out=hidden[j][:, :tiles, :],
+                in0=acc[j][:, :tiles, :],
+                in1=bias_all[:, h : h + 1, :].to_broadcast([P, tiles, DIM]),
                 op=ALU.add,
             )
 
         def squares(j):
             result[j] = result_pool.tile([P, PAIR, DIM], F32, name="result", tag="result")
             sumsq[j] = stats.tile([P, PAIR], F32, name="sumsq", tag="sumsq")
-            for m in range(PAIR):
+            for m in range(groups[j][3]):
                 nc.scalar.activation(
                     out=result[j][:, m, :],
                     in_=hidden[j][:, m, :],
@@ -222,46 +230,47 @@ def tile_gat_pa_kernel(tc, x, W1, b1, W2, b2, W3, b3, out):
                 )
 
         def invert_norms(j):
+            tiles = groups[j][3]
             clamped[j] = stats.tile([P, PAIR], F32, name="clamped", tag="clamped")
             nc.gpsimd.tensor_scalar(
-                out=clamped[j][:], in0=sumsq[j][:], scalar1=EPS * EPS, scalar2=None, op0=ALU.max
+                out=clamped[j][:, :tiles],
+                in0=sumsq[j][:, :tiles],
+                scalar1=EPS * EPS,
+                scalar2=None,
+                op0=ALU.max,
             )
             inv_norm[j] = stats.tile([P, PAIR], F32, name="inv_norm", tag="inv_norm")
             nc.scalar.activation(
-                out=inv_norm[j][:], in_=clamped[j][:], func=ACT.Abs_reciprocal_sqrt
+                out=inv_norm[j][:, :tiles],
+                in_=clamped[j][:, :tiles],
+                func=ACT.Abs_reciprocal_sqrt,
             )
 
         def scale_and_store(j):
-            c, h, first_node = place(j)
-            if j == N_PAIRS - 1:
-                nc.vector.tensor_scalar(
-                    out=result[j][:, 0, :],
-                    in0=hidden[j][:, 0, :],
-                    scalar1=inv_norm[j][:, 0:1],
-                    scalar2=None,
-                    op0=ALU.mult,
-                )
-            else:
-                nc.gpsimd.tensor_scalar(
-                    out=result[j][:, 0, :],
-                    in0=hidden[j][:, 0, :],
-                    scalar1=inv_norm[j][:, 0:1],
-                    scalar2=0.0,
-                    op0=ALU.mult,
-                    op1=ALU.add,
-                )
-            nc.vector.tensor_scalar(
-                out=result[j][:, 1, :],
-                in0=hidden[j][:, 1, :],
-                scalar1=inv_norm[j][:, 1:2],
-                scalar2=None,
-                op0=ALU.mult,
-            )
+            c, h, first_node, tiles = groups[j]
+            for m in range(tiles):
+                if m == 0 and j < VECTOR_ALONE_FROM:
+                    nc.gpsimd.tensor_scalar(
+                        out=result[j][:, m, :],
+                        in0=hidden[j][:, m, :],
+                        scalar1=inv_norm[j][:, m : m + 1],
+                        scalar2=0.0,
+                        op0=ALU.mult,
+                        op1=ALU.add,
+                    )
+                else:
+                    nc.vector.tensor_scalar(
+                        out=result[j][:, m, :],
+                        in0=hidden[j][:, m, :],
+                        scalar1=inv_norm[j][:, m : m + 1],
+                        scalar2=None,
+                        op0=ALU.mult,
+                    )
             nc.sync.dma_start(
-                out=out[h, first_node : first_node + PAIR * P, :].rearrange(
+                out=out[h, first_node : first_node + tiles * P, :].rearrange(
                     "(m p) d -> p m d", p=P
                 ),
-                in_=result[j][:],
+                in_=result[j][:, :tiles, :],
             )
 
         regroup_x_vector(0, 0)
@@ -287,7 +296,7 @@ def tile_gat_pa_kernel(tc, x, W1, b1, W2, b2, W3, b3, out):
         bias_copy(2)
         quantise_w(1, 0)
 
-        for step in range(N_PAIRS + SCALE_AFTER):
+        for step in range(n_groups + SCALE_AFTER):
             if step == 3:
                 quantise_w(2, 0)
                 quantise_w(2, 1)
@@ -295,10 +304,10 @@ def tile_gat_pa_kernel(tc, x, W1, b1, W2, b2, W3, b3, out):
             if step == 0:
                 transpose_w(2, 0)
                 transpose_w(2, 1)
-            if step < N_PAIRS:
+            if step < n_groups:
                 add_bias(step)
                 squares(step)
-            if 1 <= step <= N_PAIRS:
+            if 1 <= step <= n_groups:
                 invert_norms(step - 1)
             if step == 0:
                 empty_w(2, 0)

@@ -218,32 +218,35 @@ def tile_gat_pa_kernel(tc, x, W1, b1, W2, b2, W3, b3, out):
                 op=ALU.add,
             )
 
-        def squares(j):
-            result[j] = result_pool.tile([P, PAIR, DIM], F32, name="result", tag="result")
-            sumsq[j] = stats.tile([P, PAIR], F32, name="sumsq", tag="sumsq")
-            for m in range(groups[j][3]):
-                nc.scalar.activation(
-                    out=result[j][:, m, :],
-                    in_=hidden[j][:, m, :],
-                    func=ACT.Square,
-                    accum_out=sumsq[j][:, m : m + 1],
-                )
+        def square(j, m):
+            if m == 0:
+                result[j] = result_pool.tile([P, PAIR, DIM], F32, name="result", tag="result")
+                sumsq[j] = stats.tile([P, PAIR], F32, name="sumsq", tag="sumsq")
+            nc.scalar.activation(
+                out=result[j][:, m, :],
+                in_=hidden[j][:, m, :],
+                func=ACT.Square,
+                accum_out=sumsq[j][:, m : m + 1],
+            )
 
-        def invert_norms(j):
+        def excess(j):
             tiles = groups[j][3]
             clamped[j] = stats.tile([P, PAIR], F32, name="clamped", tag="clamped")
-            nc.gpsimd.tensor_scalar(
+            nc.scalar.activation(
                 out=clamped[j][:, :tiles],
-                in0=sumsq[j][:, :tiles],
-                scalar1=EPS * EPS,
-                scalar2=None,
-                op0=ALU.max,
+                in_=sumsq[j][:, :tiles],
+                func=ACT.Relu,
+                bias=-EPS * EPS,
             )
+
+        def root(j):
+            tiles = groups[j][3]
             inv_norm[j] = stats.tile([P, PAIR], F32, name="inv_norm", tag="inv_norm")
             nc.scalar.activation(
                 out=inv_norm[j][:, :tiles],
                 in_=clamped[j][:, :tiles],
                 func=ACT.Abs_reciprocal_sqrt,
+                bias=EPS * EPS,
             )
 
         def scale_and_store(j):
@@ -306,9 +309,13 @@ def tile_gat_pa_kernel(tc, x, W1, b1, W2, b2, W3, b3, out):
                 transpose_w(2, 1)
             if step < n_groups:
                 add_bias(step)
-                squares(step)
+                square(step, 0)
             if 1 <= step <= n_groups:
-                invert_norms(step - 1)
+                excess(step - 1)
+            if step < n_groups and groups[step][3] == PAIR:
+                square(step, 1)
+            if 1 <= step <= n_groups:
+                root(step - 1)
             if step == 0:
                 empty_w(2, 0)
                 empty_w(2, 1)

@@ -44,7 +44,7 @@ def tile_gat_pa_kernel(tc, x, W1, b1, W2, b2, W3, b3, out):
         name="stats", bufs=6
     ) as stats, tc.psum_pool(name="wt_psum", bufs=2) as wt_psum, tc.psum_pool(
         name="acc_psum", bufs=4
-    ) as acc_psum, ExitStack() as ctx:
+    ) as acc_psum, tc.psum_pool(name="idle_psum", bufs=1) as idle_psum, ExitStack() as ctx:
         ctx.enter_context(tc.manual_schedule())
 
         bias_rows = keep.tile([P, HEADS, DIM], BF16, name="bias_rows")
@@ -86,6 +86,16 @@ def tile_gat_pa_kernel(tc, x, W1, b1, W2, b2, W3, b3, out):
         load_w(2)
         load_x(0, 1)
         load_x(1, 1)
+
+        idle = idle_psum.tile([P, P], F32, name="idle")
+
+        def keep_warm(times):
+            for i in range(times):
+                nc.tensor.matmul(
+                    out=idle[:], lhsT=ident[:], rhs=ident[:], start=True, stop=True
+                )
+
+        keep_warm(9)
 
         bias_all = keep.tile([P, HEADS, DIM], F32, name="bias_all")
         bias_ps = {}
@@ -280,6 +290,7 @@ def tile_gat_pa_kernel(tc, x, W1, b1, W2, b2, W3, b3, out):
         regroup_x_scalar(0, 0)
         transpose_w(0, 0)
         transpose_w(0, 1)
+        keep_warm(2)
         empty_w(0, 0)
         quantise_x(0, 0)
         regroup_x_vector(1, 0)
@@ -288,8 +299,10 @@ def tile_gat_pa_kernel(tc, x, W1, b1, W2, b2, W3, b3, out):
         quantise_w(0, 0)
         for h in range(HEADS):
             bias_matmul(h)
+        keep_warm(2)
         transpose_w(1, 0)
         transpose_w(1, 1)
+        keep_warm(2)
         bias_copy(0)
         quantise_x(1, 0)
         quantise_w(0, 1)

@@ -87,15 +87,17 @@ def tile_gat_pa_kernel(tc, x, W1, b1, W2, b2, W3, b3, out):
         load_x(0, 1)
         load_x(1, 1)
 
-        idle = idle_psum.tile([P, P], F32, name="idle")
+        idle = idle_psum.tile([P, X_CHUNK], F32, name="idle")
 
-        def keep_warm(times):
-            for i in range(times):
-                nc.tensor.matmul(
-                    out=idle[:], lhsT=ident[:], rhs=ident[:], start=True, stop=True
-                )
+        def keep_warm():
+            nc.tensor.matmul(
+                out=idle[:], lhsT=ones[:], rhs=x_raw[0, 0][:, 0, :], start=True, stop=True
+            )
 
-        keep_warm(9)
+        for i in range(6):
+            nc.tensor.matmul(
+                out=idle[:, :P], lhsT=ident[:], rhs=ident[:], start=True, stop=True
+            )
 
         bias_all = keep.tile([P, HEADS, DIM], F32, name="bias_all")
         bias_ps = {}
@@ -290,7 +292,7 @@ def tile_gat_pa_kernel(tc, x, W1, b1, W2, b2, W3, b3, out):
         regroup_x_scalar(0, 0)
         transpose_w(0, 0)
         transpose_w(0, 1)
-        keep_warm(2)
+        keep_warm()
         empty_w(0, 0)
         quantise_x(0, 0)
         regroup_x_vector(1, 0)
@@ -299,10 +301,9 @@ def tile_gat_pa_kernel(tc, x, W1, b1, W2, b2, W3, b3, out):
         quantise_w(0, 0)
         for h in range(HEADS):
             bias_matmul(h)
-        keep_warm(2)
         transpose_w(1, 0)
         transpose_w(1, 1)
-        keep_warm(2)
+        keep_warm()
         bias_copy(0)
         quantise_x(1, 0)
         quantise_w(0, 1)

@@ -89,12 +89,13 @@ def tile_gat_pa_kernel(tc, x, W1, b1, W2, b2, W3, b3, out):
 
         idle = idle_psum.tile([P, X_CHUNK], F32, name="idle")
 
-        def keep_warm():
-            nc.tensor.matmul(
-                out=idle[:], lhsT=ones[:], rhs=x_raw[0, 0][:, 0, :], start=True, stop=True
-            )
+        def keep_warm(times):
+            for i in range(times):
+                nc.tensor.matmul(
+                    out=idle[:], lhsT=ones[:], rhs=x_raw[0, 0][:, i, :], start=True, stop=True
+                )
 
-        for i in range(6):
+        for i in range(7):
             nc.tensor.matmul(
                 out=idle[:, :P], lhsT=ident[:], rhs=ident[:], start=True, stop=True
             )
@@ -292,7 +293,7 @@ def tile_gat_pa_kernel(tc, x, W1, b1, W2, b2, W3, b3, out):
         regroup_x_scalar(0, 0)
         transpose_w(0, 0)
         transpose_w(0, 1)
-        keep_warm()
+        keep_warm(2)
         empty_w(0, 0)
         quantise_x(0, 0)
         regroup_x_vector(1, 0)
@@ -301,9 +302,10 @@ def tile_gat_pa_kernel(tc, x, W1, b1, W2, b2, W3, b3, out):
         quantise_w(0, 0)
         for h in range(HEADS):
             bias_matmul(h)
+        keep_warm(1)
         transpose_w(1, 0)
         transpose_w(1, 1)
-        keep_warm()
+        keep_warm(2)
         bias_copy(0)
         quantise_x(1, 0)
         quantise_w(0, 1)

@@ -24,11 +24,14 @@ FLOPS = 2 * NODES * FEATURES * HEADS * DIM
 
 X_CHUNK = 512
 X_CHUNKS = NODES // X_CHUNK
-X_VECTOR_NODES = 320
+X_VECTOR_NODES = {(0, 0): 384, (1, 0): 448, (0, 1): 320, (1, 1): 320}
 PAIR = 2
 PAIRS_PER_CHUNK = X_CHUNK // (PAIR * P)
 N_PAIRS = X_CHUNKS * HEADS * PAIRS_PER_CHUNK
-SCALE_AFTER = 3
+SCALE_AFTER = 4
+LAST_SCALE_AFTER = 2
+NORM_BLOCK = 2
+SINGLE_NORMS = 3
 VECTOR_ALONE_FROM = 7
 
 
@@ -39,9 +42,9 @@ def tile_gat_pa_kernel(tc, x, W1, b1, W2, b2, W3, b3, out):
     x_rows = x.rearrange("b f i j -> (b f) (i j)")
 
     with tc.tile_pool(name="keep", bufs=1) as keep, tc.tile_pool(
-        name="hidden_pool", bufs=6
-    ) as hidden_pool, tc.tile_pool(name="result_pool", bufs=8) as result_pool, tc.tile_pool(
-        name="stats", bufs=6
+        name="hidden_pool", bufs=13
+    ) as hidden_pool, tc.tile_pool(name="result_pool", bufs=13) as result_pool, tc.tile_pool(
+        name="stats", bufs=13
     ) as stats, tc.psum_pool(name="wt_psum", bufs=2) as wt_psum, tc.psum_pool(
         name="acc_psum", bufs=4
     ) as acc_psum, tc.psum_pool(name="idle_psum", bufs=1) as idle_psum, ExitStack() as ctx:
@@ -100,23 +103,25 @@ def tile_gat_pa_kernel(tc, x, W1, b1, W2, b2, W3, b3, out):
                 out=idle[:, :P], lhsT=ident[:], rhs=ident[:], start=True, stop=True
             )
 
-        bias_all = keep.tile([P, HEADS, DIM], F32, name="bias_all")
-        bias_ps = {}
+        bias_all = keep.tile([P, HEADS, DIM], BF16, name="bias_all")
+        bias_ps = acc_psum.tile([P, HEADS, DIM], BF16, name="bias_ps", tag="acc")
 
-        def bias_matmul(h):
-            bias_ps[h] = acc_psum.tile([P, DIM], F32, name="bias_ps", tag="acc")
+        def bias_matmul(first, last):
             nc.tensor.matmul(
-                out=bias_ps[h][:], lhsT=ones[:], rhs=bias_rows[:, h, :], start=True, stop=True
+                out=bias_ps[:, first:last, :],
+                lhsT=ones[:],
+                rhs=bias_rows[:, first:last, :],
+                start=True,
+                stop=True,
             )
 
-        def bias_copy(h):
-            nc.scalar.copy(out=bias_all[:, h, :], in_=bias_ps[h][:])
+        def bias_copy():
+            nc.scalar.copy(out=bias_all[:], in_=bias_ps[:])
 
         x_codes = keep.tile([P, PASSES, NODES], U32, name="x_codes", align_bytes=64)
         x_scales = keep.tile([P, PASSES, NODES], U8, name="x_scales", align_bytes=64)
         x_grouped = {}
         quantised = set()
-        cut = X_VECTOR_NODES // 4
 
         def grouped_views(g, c):
             if (g, c) not in x_grouped:
@@ -129,10 +134,12 @@ def tile_gat_pa_kernel(tc, x, W1, b1, W2, b2, W3, b3, out):
 
         def regroup_x_vector(g, c):
             dst, src = grouped_views(g, c)
+            cut = X_VECTOR_NODES[g, c] // 4
             nc.vector.tensor_copy(out=dst[:, :cut], in_=src[:, :cut])
 
         def regroup_x_scalar(g, c):
             dst, src = grouped_views(g, c)
+            cut = X_VECTOR_NODES[g, c] // 4
             nc.scalar.copy(out=dst[:, cut:], in_=src[:, cut:])
 
         def quantise_x(g, c):
@@ -199,6 +206,15 @@ def tile_gat_pa_kernel(tc, x, W1, b1, W2, b2, W3, b3, out):
                     groups.append((c, h, first_node + m * P, 1))
         n_groups = len(groups)
 
+        norm_block = {}
+        block_start = 0
+        while block_start < n_groups:
+            size = NORM_BLOCK if block_start + NORM_BLOCK <= n_groups - SINGLE_NORMS else 1
+            members = tuple(range(block_start, block_start + size))
+            for position, member in enumerate(members):
+                norm_block[member] = (members, position * PAIR)
+            block_start += size
+
         def matmuls(j):
             if j >= n_groups or j in acc:
                 return
@@ -234,42 +250,58 @@ def tile_gat_pa_kernel(tc, x, W1, b1, W2, b2, W3, b3, out):
         def square(j, m):
             if m == 0:
                 result[j] = result_pool.tile([P, PAIR, DIM], F32, name="result", tag="result")
-                sumsq[j] = stats.tile([P, PAIR], F32, name="sumsq", tag="sumsq")
+            members, column = norm_block[j]
+            if m == 0 and column == 0:
+                sumsq[members] = stats.tile(
+                    [P, NORM_BLOCK * PAIR], F32, name="sumsq", tag="sumsq"
+                )
             nc.scalar.activation(
                 out=result[j][:, m, :],
                 in_=hidden[j][:, m, :],
                 func=ACT.Square,
-                accum_out=sumsq[j][:, m : m + 1],
+                accum_out=sumsq[members][:, column + m : column + m + 1],
             )
 
         def excess(j):
-            tiles = groups[j][3]
-            clamped[j] = stats.tile([P, PAIR], F32, name="clamped", tag="clamped")
+            members, column = norm_block[j]
+            if j != members[-1]:
+                return
+            columns = column + groups[j][3]
+            clamped[members] = stats.tile(
+                [P, NORM_BLOCK * PAIR], F32, name="clamped", tag="clamped"
+            )
             nc.scalar.activation(
-                out=clamped[j][:, :tiles],
-                in_=sumsq[j][:, :tiles],
+                out=clamped[members][:, :columns],
+                in_=sumsq[members][:, :columns],
                 func=ACT.Relu,
                 bias=-EPS * EPS,
             )
 
         def root(j):
-            tiles = groups[j][3]
-            inv_norm[j] = stats.tile([P, PAIR], F32, name="inv_norm", tag="inv_norm")
+            members, column = norm_block[j]
+            if j != members[-1]:
+                return
+            columns = column + groups[j][3]
+            inv_norm[members] = stats.tile(
+                [P, NORM_BLOCK * PAIR], F32, name="inv_norm", tag="inv_norm"
+            )
             nc.scalar.activation(
-                out=inv_norm[j][:, :tiles],
-                in_=clamped[j][:, :tiles],
+                out=inv_norm[members][:, :columns],
+                in_=clamped[members][:, :columns],
                 func=ACT.Abs_reciprocal_sqrt,
                 bias=EPS * EPS,
             )
 
         def scale_and_store(j):
             c, h, first_node, tiles = groups[j]
+            members, column = norm_block[j]
+            inverse = inv_norm[members]
             for m in range(tiles):
                 if m == 0 and j < VECTOR_ALONE_FROM:
                     nc.gpsimd.tensor_scalar(
                         out=result[j][:, m, :],
                         in0=hidden[j][:, m, :],
-                        scalar1=inv_norm[j][:, m : m + 1],
+                        scalar1=inverse[:, column + m : column + m + 1],
                         scalar2=0.0,
                         op0=ALU.mult,
                         op1=ALU.add,
@@ -278,7 +310,7 @@ def tile_gat_pa_kernel(tc, x, W1, b1, W2, b2, W3, b3, out):
                     nc.vector.tensor_scalar(
                         out=result[j][:, m, :],
                         in0=hidden[j][:, m, :],
-                        scalar1=inv_norm[j][:, m : m + 1],
+                        scalar1=inverse[:, column + m : column + m + 1],
                         scalar2=None,
                         op0=ALU.mult,
                     )
@@ -293,33 +325,32 @@ def tile_gat_pa_kernel(tc, x, W1, b1, W2, b2, W3, b3, out):
         regroup_x_scalar(0, 0)
         transpose_w(0, 0)
         transpose_w(0, 1)
-        keep_warm(2)
+        keep_warm(1)
         empty_w(0, 0)
         quantise_x(0, 0)
         regroup_x_vector(1, 0)
         regroup_x_scalar(1, 0)
         empty_w(0, 1)
         quantise_w(0, 0)
-        for h in range(HEADS):
-            bias_matmul(h)
+        bias_matmul(0, 2)
+        bias_matmul(2, HEADS)
         keep_warm(1)
         transpose_w(1, 0)
         transpose_w(1, 1)
-        keep_warm(2)
-        bias_copy(0)
+        bias_copy()
         quantise_x(1, 0)
         quantise_w(0, 1)
         empty_w(1, 0)
         empty_w(1, 1)
-        bias_copy(1)
-        bias_copy(2)
         quantise_w(1, 0)
 
-        for step in range(n_groups + SCALE_AFTER):
+        scaled = 0
+        for step in range(n_groups + LAST_SCALE_AFTER):
             if step == 3:
                 quantise_w(2, 0)
                 quantise_w(2, 1)
             matmuls(step)
+            matmuls(step + 1)
             if step == 0:
                 transpose_w(2, 0)
                 transpose_w(2, 1)
@@ -337,8 +368,10 @@ def tile_gat_pa_kernel(tc, x, W1, b1, W2, b2, W3, b3, out):
                 empty_w(2, 1)
             if step == 1 or step == 2:
                 regroup_x_scalar(step - 1, 1)
-            if step >= SCALE_AFTER:
-                scale_and_store(step - SCALE_AFTER)
+            distance = max(LAST_SCALE_AFTER, min(SCALE_AFTER, n_groups - step))
+            while scaled <= step - distance:
+                scale_and_store(scaled)
+                scaled += 1
             if step == 0:
                 quantise_w(1, 1)
                 regroup_x_vector(0, 1)
@@ -346,5 +379,4 @@ def tile_gat_pa_kernel(tc, x, W1, b1, W2, b2, W3, b3, out):
                 regroup_x_vector(1, 1)
             if step == 3 or step == 4:
                 quantise_x(step - 3, 1)
-            matmuls(step + 1)
             matmuls(step + 2)

@@ -86,8 +86,8 @@ def tile_gat_pa_kernel(tc, x, W1, b1, W2, b2, W3, b3, out):
                 out=bias_rows[0:1, h, :], in_=biases[h].rearrange("(o d) -> o d", o=1)
             )
         load_w(1)
-        load_w(2)
         load_x(0, 1)
+        load_w(2)
         load_x(1, 1)
 
         idle = idle_psum.tile([P, X_CHUNK], F32, name="idle")
@@ -334,7 +334,6 @@ def tile_gat_pa_kernel(tc, x, W1, b1, W2, b2, W3, b3, out):
         quantise_w(0, 0)
         bias_matmul(0, 2)
         bias_matmul(2, HEADS)
-        keep_warm(1)
         transpose_w(1, 0)
         transpose_w(1, 1)
         bias_copy()
@@ -346,16 +345,23 @@ def tile_gat_pa_kernel(tc, x, W1, b1, W2, b2, W3, b3, out):
 
         scaled = 0
         for step in range(n_groups + LAST_SCALE_AFTER):
-            if step == 3:
-                quantise_w(2, 0)
-                quantise_w(2, 1)
             matmuls(step)
             matmuls(step + 1)
             if step == 0:
                 transpose_w(2, 0)
                 transpose_w(2, 1)
+            if step == 0:
+                regroup_x_scalar(0, 1)
+            if step == 1:
+                empty_w(2, 0)
+                empty_w(2, 1)
+            if step == 3:
+                regroup_x_scalar(1, 1)
             if step < n_groups:
                 add_bias(step)
+            if step == 0:
+                quantise_w(1, 1)
+            if step < n_groups:
                 square(step, 0)
             if 1 <= step <= n_groups:
                 excess(step - 1)
@@ -363,20 +369,17 @@ def tile_gat_pa_kernel(tc, x, W1, b1, W2, b2, W3, b3, out):
                 square(step, 1)
             if 1 <= step <= n_groups:
                 root(step - 1)
-            if step == 0:
-                empty_w(2, 0)
-                empty_w(2, 1)
-            if step == 1 or step == 2:
-                regroup_x_scalar(step - 1, 1)
+            if step == 4:
+                quantise_x(1, 1)
             distance = max(LAST_SCALE_AFTER, min(SCALE_AFTER, n_groups - step))
             while scaled <= step - distance:
                 scale_and_store(scaled)
                 scaled += 1
-            if step == 0:
-                quantise_w(1, 1)
+            if step == 1:
                 regroup_x_vector(0, 1)
-            if step == 2:
                 regroup_x_vector(1, 1)
-            if step == 3 or step == 4:
-                quantise_x(step - 3, 1)
+            if step == 2:
+                quantise_w(2, 0)
+                quantise_w(2, 1)
+                quantise_x(0, 1)
             matmuls(step + 2)

@@ -24,14 +24,14 @@ FLOPS = 2 * NODES * FEATURES * HEADS * DIM
 
 X_CHUNK = 512
 X_CHUNKS = NODES // X_CHUNK
-X_VECTOR_NODES = {(0, 0): 384, (1, 0): 448, (0, 1): 320, (1, 1): 320}
+X_VECTOR_NODES = {(0, 0): 384, (1, 0): 416, (0, 1): 288, (1, 1): 320}
 PAIR = 2
 PAIRS_PER_CHUNK = X_CHUNK // (PAIR * P)
 N_PAIRS = X_CHUNKS * HEADS * PAIRS_PER_CHUNK
 SCALE_AFTER = 4
 LAST_SCALE_AFTER = 2
 NORM_BLOCK = 2
-SINGLE_NORMS = 3
+SINGLE_NORMS = 5
 VECTOR_ALONE_FROM = 7
 
 
@@ -341,6 +341,7 @@ def tile_gat_pa_kernel(tc, x, W1, b1, W2, b2, W3, b3, out):
         quantise_w(0, 1)
         empty_w(1, 0)
         empty_w(1, 1)
+        regroup_x_vector(0, 1)
         quantise_w(1, 0)
 
         scaled = 0
@@ -376,7 +377,6 @@ def tile_gat_pa_kernel(tc, x, W1, b1, W2, b2, W3, b3, out):
                 scale_and_store(scaled)
                 scaled += 1
             if step == 1:
-                regroup_x_vector(0, 1)
                 regroup_x_vector(1, 1)
             if step == 2:
                 quantise_w(2, 0)

@@ -358,8 +358,10 @@ def tile_gat_pa_kernel(tc, x, W1, b1, W2, b2, W3, b3, out):
                 empty_w(2, 1)
             if step == 3:
                 regroup_x_scalar(1, 1)
-            if step < n_groups:
+            if step < n_groups and step not in hidden:
                 add_bias(step)
+            if step == n_groups - 2:
+                add_bias(step + 1)
             if step == 0:
                 quantise_w(1, 1)
             if step < n_groups:

from contextlib import ExitStack

import concourse.mybir as mybir
from concourse.masks import make_identity

F32 = mybir.dt.float32
BF16 = mybir.dt.bfloat16
U32 = mybir.dt.uint32
U8 = mybir.dt.uint8
FP8X4 = mybir.dt.float8_e4m3fn_x4
ALU = mybir.AluOpType
ACT = mybir.ActivationFunctionType

P = 128
PACK = 4
K_PASS = P * PACK
FEATURES = 1024
NODES = 1024
DIM = 256
HEADS = 3
PASSES = FEATURES // K_PASS
EPS = 1e-12
FLOPS = 2 * NODES * FEATURES * HEADS * DIM

X_CHUNK = 512
X_CHUNKS = NODES // X_CHUNK
X_VECTOR_NODES = {(0, 0): 384, (1, 0): 416, (0, 1): 288, (1, 1): 320}
PAIR = 2
PAIRS_PER_CHUNK = X_CHUNK // (PAIR * P)
N_PAIRS = X_CHUNKS * HEADS * PAIRS_PER_CHUNK
SCALE_AFTER = 4
LAST_SCALE_AFTER = 2
NORM_BLOCK = 2
SINGLE_NORMS = 5
VECTOR_ALONE_FROM = 7


def tile_gat_pa_kernel(tc, x, W1, b1, W2, b2, W3, b3, out):
    nc = tc.nc
    weights = (W1, W2, W3)
    biases = (b1, b2, b3)
    x_rows = x.rearrange("b f i j -> (b f) (i j)")

    with tc.tile_pool(name="keep", bufs=1) as keep, tc.tile_pool(
        name="hidden_pool", bufs=13
    ) as hidden_pool, tc.tile_pool(name="result_pool", bufs=13) as result_pool, tc.tile_pool(
        name="stats", bufs=13
    ) as stats, tc.psum_pool(name="wt_psum", bufs=2) as wt_psum, tc.psum_pool(
        name="acc_psum", bufs=4
    ) as acc_psum, tc.psum_pool(name="idle_psum", bufs=1) as idle_psum, ExitStack() as ctx:
        ctx.enter_context(tc.manual_schedule())

        bias_rows = keep.tile([P, HEADS, DIM], BF16, name="bias_rows")
        nc.vector.memset(bias_rows[:], 0.0)
        ident = keep.tile([P, P], F32, name="ident")
        make_identity(nc, ident[:])
        ones = keep.tile([P, P], BF16, name="ones")
        nc.vector.memset(ones[:], 1.0)
        warm = keep.tile([P, 1], F32, name="warm")
        nc.vector.memset(warm[:], 1.0)
        nc.scalar.activation(out=warm[:], in_=warm[:], func=ACT.Abs_reciprocal_sqrt)

        x_raw = {}
        w_raw = {}

        def load_x(g, c):
            x_raw[g, c] = keep.tile([P, PACK, X_CHUNK], BF16, name="x_raw%d_%d" % (g, c))
            nc.sync.dma_start(
                out=x_raw[g, c][:],
                in_=x_rows[
                    g * K_PASS : (g + 1) * K_PASS, c * X_CHUNK : (c + 1) * X_CHUNK
                ].rearrange("(p t) n -> p t n", t=PACK),
            )

        def load_w(h):
            w_raw[h] = keep.tile([P, 2 * FEATURES], BF16, name="w_raw%d" % h)
            nc.sync.dma_start(
                out=w_raw[h][:], in_=weights[h].rearrange("(m r) k -> m (r k)", r=2)
            )

        load_x(0, 0)
        load_w(0)
        load_x(1, 0)
        for h in range(HEADS):
            nc.sync.dma_start(
                out=bias_rows[0:1, h, :], in_=biases[h].rearrange("(o d) -> o d", o=1)
            )
        load_w(1)
        load_x(0, 1)
        load_w(2)
        load_x(1, 1)

        idle = idle_psum.tile([P, X_CHUNK], F32, name="idle")

        def keep_warm(times):
            for i in range(times):
                nc.tensor.matmul(
                    out=idle[:], lhsT=ones[:], rhs=x_raw[0, 0][:, i, :], start=True, stop=True
                )

        for i in range(7):
            nc.tensor.matmul(
                out=idle[:, :P], lhsT=ident[:], rhs=ident[:], start=True, stop=True
            )

        bias_all = keep.tile([P, HEADS, DIM], BF16, name="bias_all")
        bias_ps = acc_psum.tile([P, HEADS, DIM], BF16, name="bias_ps", tag="acc")

        def bias_matmul(first, last):
            nc.tensor.matmul(
                out=bias_ps[:, first:last, :],
                lhsT=ones[:],
                rhs=bias_rows[:, first:last, :],
                start=True,
                stop=True,
            )

        def bias_copy():
            nc.scalar.copy(out=bias_all[:], in_=bias_ps[:])

        x_codes = keep.tile([P, PASSES, NODES], U32, name="x_codes", align_bytes=64)
        x_scales = keep.tile([P, PASSES, NODES], U8, name="x_scales", align_bytes=64)
        x_grouped = {}
        quantised = set()

        def grouped_views(g, c):
            if (g, c) not in x_grouped:
                x_grouped[g, c] = keep.tile(
                    [P, X_CHUNK, PACK], BF16, name="x_grouped%d_%d" % (g, c), align_bytes=64
                )
            dst = x_grouped[g, c][:].rearrange("p (c i) t -> p c t i", i=4)
            src = x_raw[g, c][:].rearrange("p t (c i) -> p c t i", i=4)
            return dst, src

        def regroup_x_vector(g, c):
            dst, src = grouped_views(g, c)
            cut = X_VECTOR_NODES[g, c] // 4
            nc.vector.tensor_copy(out=dst[:, :cut], in_=src[:, :cut])

        def regroup_x_scalar(g, c):
            dst, src = grouped_views(g, c)
            cut = X_VECTOR_NODES[g, c] // 4
            nc.scalar.copy(out=dst[:, cut:], in_=src[:, cut:])

        def quantise_x(g, c):
            nodes = slice(c * X_CHUNK, (c + 1) * X_CHUNK)
            nc.vector.quantize_mx(
                out=x_codes[:, g, nodes].bitcast(FP8X4),
                scales=x_scales[:, g, nodes],
                in_=x_grouped[g, c][:].rearrange("p n t -> p (n t)"),
            )
            quantised.add(("x", g, c))

        w_codes = keep.tile([P, HEADS, PASSES, DIM], U32, name="w_codes", align_bytes=64)
        w_scales = keep.tile([P, HEADS, PASSES, DIM], U8, name="w_scales", align_bytes=64)
        w_grouped = {}
        w_turned = {}

        def transpose_w(h, g):
            words = w_raw[h][:].bitcast(F32).rearrange("m (r w) -> m r w", r=2)
            w_turned[h, g] = wt_psum.tile([P, 2, 2, P], F32, name="wt", tag="wt")
            for r in range(2):
                for u in range(2):
                    nc.tensor.transpose(
                        w_turned[h, g][:, r, u, :],
                        words[:, r, 256 * g + u : 256 * (g + 1) : 2],
                        ident[:],
                    )

        def empty_w(h, g):
            if h not in w_grouped:
                w_grouped[h] = keep.tile(
                    [P, PASSES * DIM * PACK], BF16, name="w_grouped%d" % h, align_bytes=64
                )
            grouped_words = w_grouped[h][:].bitcast(F32).rearrange(
                "p (g m r u) -> p g m r u", g=PASSES, r=2, u=2
            )
            nc.scalar.copy(
                out=grouped_words[:, g], in_=w_turned[h, g][:].rearrange("p r u m -> p m r u")
            )

        def quantise_w(h, g):
            nc.vector.quantize_mx(
                out=w_codes[:, h, g, :].bitcast(FP8X4),
                scales=w_scales[:, h, g, :],
                in_=w_grouped[h][:, g * DIM * PACK : (g + 1) * DIM * PACK],
            )
            quantised.add(("w", h, g))

        acc = {}
        hidden = {}
        result = {}
        sumsq = {}
        clamped = {}
        inv_norm = {}

        groups = []
        for j in range(N_PAIRS):
            c, rest = divmod(j, HEADS * PAIRS_PER_CHUNK)
            h, i = divmod(rest, PAIRS_PER_CHUNK)
            first_node = c * X_CHUNK + i * PAIR * P
            if j < N_PAIRS - 1:
                groups.append((c, h, first_node, PAIR))
            else:
                for m in range(PAIR):
                    groups.append((c, h, first_node + m * P, 1))
        n_groups = len(groups)

        norm_block = {}
        block_start = 0
        while block_start < n_groups:
            size = NORM_BLOCK if block_start + NORM_BLOCK <= n_groups - SINGLE_NORMS else 1
            members = tuple(range(block_start, block_start + size))
            for position, member in enumerate(members):
                norm_block[member] = (members, position * PAIR)
            block_start += size

        def matmuls(j):
            if j >= n_groups or j in acc:
                return
            c, h, first_node, tiles = groups[j]
            if not all(
                ("x", g, c) in quantised and ("w", h, g) in quantised for g in range(PASSES)
            ):
                return
            acc[j] = acc_psum.tile([P, PAIR, DIM], F32, name="acc", tag="acc")
            for m in range(tiles):
                nodes = slice(first_node + m * P, first_node + (m + 1) * P)
                for g in range(PASSES):
                    nc.tensor.matmul_mx(
                        out=acc[j][:, m, :],
                        lhsT=x_codes[:, g, nodes].bitcast(FP8X4),
                        lhsT_scale=x_scales[:, g, nodes],
                        rhs=w_codes[:, h, g, :].bitcast(FP8X4),
                        rhs_scale=w_scales[:, h, g, :],
                        start=(g == 0),
                        stop=(g == PASSES - 1),
                    )

        def add_bias(j):
            c, h, first_node, tiles = groups[j]
            hidden[j] = hidden_pool.tile([P, PAIR, DIM], F32, name="hidden", tag="hidden")
            nc.vector.tensor_tensor(
                out=hidden[j][:, :tiles, :],
                in0=acc[j][:, :tiles, :],
                in1=bias_all[:, h : h + 1, :].to_broadcast([P, tiles, DIM]),
                op=ALU.add,
            )

        def square(j, m):
            if m == 0:
                result[j] = result_pool.tile([P, PAIR, DIM], F32, name="result", tag="result")
            members, column = norm_block[j]
            if m == 0 and column == 0:
                sumsq[members] = stats.tile(
                    [P, NORM_BLOCK * PAIR], F32, name="sumsq", tag="sumsq"
                )
            nc.scalar.activation(
                out=result[j][:, m, :],
                in_=hidden[j][:, m, :],
                func=ACT.Square,
                accum_out=sumsq[members][:, column + m : column + m + 1],
            )

        def excess(j):
            members, column = norm_block[j]
            if j != members[-1]:
                return
            columns = column + groups[j][3]
            clamped[members] = stats.tile(
                [P, NORM_BLOCK * PAIR], F32, name="clamped", tag="clamped"
            )
            nc.scalar.activation(
                out=clamped[members][:, :columns],
                in_=sumsq[members][:, :columns],
                func=ACT.Relu,
                bias=-EPS * EPS,
            )

        def root(j):
            members, column = norm_block[j]
            if j != members[-1]:
                return
            columns = column + groups[j][3]
            inv_norm[members] = stats.tile(
                [P, NORM_BLOCK * PAIR], F32, name="inv_norm", tag="inv_norm"
            )
            nc.scalar.activation(
                out=inv_norm[members][:, :columns],
                in_=clamped[members][:, :columns],
                func=ACT.Abs_reciprocal_sqrt,
                bias=EPS * EPS,
            )

        def scale_and_store(j):
            c, h, first_node, tiles = groups[j]
            members, column = norm_block[j]
            inverse = inv_norm[members]
            for m in range(tiles):
                if m == 0 and j < VECTOR_ALONE_FROM:
                    nc.gpsimd.tensor_scalar(
                        out=result[j][:, m, :],
                        in0=hidden[j][:, m, :],
                        scalar1=inverse[:, column + m : column + m + 1],
                        scalar2=0.0,
                        op0=ALU.mult,
                        op1=ALU.add,
                    )
                else:
                    nc.vector.tensor_scalar(
                        out=result[j][:, m, :],
                        in0=hidden[j][:, m, :],
                        scalar1=inverse[:, column + m : column + m + 1],
                        scalar2=None,
                        op0=ALU.mult,
                    )
            nc.sync.dma_start(
                out=out[h, first_node : first_node + tiles * P, :].rearrange(
                    "(m p) d -> p m d", p=P
                ),
                in_=result[j][:, :tiles, :],
            )

        regroup_x_vector(0, 0)
        regroup_x_scalar(0, 0)
        transpose_w(0, 0)
        transpose_w(0, 1)
        keep_warm(1)
        empty_w(0, 0)
        quantise_x(0, 0)
        regroup_x_vector(1, 0)
        regroup_x_scalar(1, 0)
        empty_w(0, 1)
        quantise_w(0, 0)
        bias_matmul(0, 2)
        bias_matmul(2, HEADS)
        transpose_w(1, 0)
        transpose_w(1, 1)
        bias_copy()
        quantise_x(1, 0)
        quantise_w(0, 1)
        empty_w(1, 0)
        empty_w(1, 1)
        regroup_x_vector(0, 1)
        quantise_w(1, 0)

        scaled = 0
        for step in range(n_groups + LAST_SCALE_AFTER):
            matmuls(step)
            matmuls(step + 1)
            if step == 0:
                transpose_w(2, 0)
                transpose_w(2, 1)
            if step == 0:
                regroup_x_scalar(0, 1)
            if step == 1:
                empty_w(2, 0)
                empty_w(2, 1)
            if step == 3:
                regroup_x_scalar(1, 1)
            if step < n_groups and step not in hidden:
                add_bias(step)
            if step == n_groups - 2:
                add_bias(step + 1)
            if step == 0:
                quantise_w(1, 1)
            if step < n_groups:
                square(step, 0)
            if 1 <= step <= n_groups:
                excess(step - 1)
            if step < n_groups and groups[step][3] == PAIR:
                square(step, 1)
            if 1 <= step <= n_groups:
                root(step - 1)
            if step == 4:
                quantise_x(1, 1)
            distance = max(LAST_SCALE_AFTER, min(SCALE_AFTER, n_groups - step))
            while scaled <= step - distance:
                scale_and_store(scaled)
                scaled += 1
            if step == 1:
                regroup_x_vector(1, 1)
            if step == 2:
                quantise_w(2, 0)
                quantise_w(2, 1)
                quantise_x(0, 1)
            matmuls(step + 2)
